import numpy as np
import ml_dtypes


def mxq(x, axis, fmt="e4m3"):
    dtype, down = {"e4m3": (ml_dtypes.float8_e4m3fn, 7), "e5m2": (ml_dtypes.float8_e5m2, 14)}[fmt]
    v = np.moveaxis(np.asarray(x, np.float32).astype(ml_dtypes.bfloat16).astype(np.float64), axis, -1)
    blocks = v.reshape(v.shape[:-1] + (-1, 32))
    amax = np.abs(blocks).max(-1, keepdims=True)
    byte = np.maximum(np.where(amax > 0, np.frexp(amax)[1] - 1 + 127, 0) - down, 1)
    scale = np.exp2(byte - 127.0)
    codes = (blocks / scale).astype(np.float32).astype(dtype).astype(np.float64)
    return np.moveaxis((codes * scale).reshape(v.shape), -1, axis)


WIDE = False


def mx_kscale(k):
    if not WIDE:
        return np.ones(k)
    levels = np.array([10, -10, 5, -5, 0])
    a = np.random.permutation(np.resize(levels, k // 512 * 4)).reshape(k // 512, 4)
    idx = np.arange(k)
    return np.exp2(a[idx // 512, idx % 128 // 32])


BF16 = ml_dtypes.bfloat16


def bf(x):
    return np.asarray(x, np.float32).astype(BF16)


def f64(x):
    return np.asarray(x).astype(np.float64)


B, I, H, S = 4096, 512, 512, 1024
LAM_DIRECT = 1.0
LAM_SPARSE = 1.0
SIG = 1.0
EPS = 0.0001
G = 1.5


def setup_inputs():
    si, sh, ss = mx_kscale(I), mx_kscale(H), mx_kscale(S)
    z = np.random.standard_normal((B, S)) * G * np.sqrt(2.0)
    e = np.exp(z - z.max(axis=1, keepdims=True))
    sy = e / e.sum(axis=1, keepdims=True)
    return {"x": bf(np.random.standard_normal((B, I)) * si),
            "hx": bf(np.random.standard_normal((B, H)) * sh),
            "sy": bf(sy * ss),
            "internal": bf(np.random.standard_normal((B, H))),
            "W_ih": bf(np.random.standard_normal((H, I)) * 0.7 / np.sqrt(I) / si),
            "W_hh": bf(np.random.standard_normal((H, H)) * 0.7 / np.sqrt(H) / sh),
            "W_sh": bf(np.random.standard_normal((H, S)) * 3.0 / ss),
            "mu": bf(np.random.standard_normal(H) * 0.3)}


def reference(x, hx, sy, internal, W_ih, W_hh, W_sh, mu):
    direct = mxq(f64(x), 1, "e4m3") @ mxq(f64(W_ih).T, 0, "e4m3")
    recur = mxq(f64(hx), 1, "e4m3") @ mxq(f64(W_hh).T, 0, "e4m3")
    sparse = mxq(f64(sy), 1, "e4m3") @ mxq(f64(W_sh).T, 0, "e4m3")
    pre = LAM_DIRECT * direct + recur + LAM_SPARSE * sparse
    m = pre.mean(-1, keepdims=True)
    sd = np.sqrt(((pre - m) ** 2).mean(-1, keepdims=True)) + EPS
    ln = (pre - m) / sd * SIG + f64(mu)
    return np.maximum(ln + f64(internal), 0.0)

@@ -1,0 +1,272 @@
+from contextlib import ExitStack
+
+import concourse.mybir as mybir
+from concourse.masks import make_identity
+
+F32 = mybir.dt.float32
+BF16 = mybir.dt.bfloat16
+U32 = mybir.dt.uint32
+U8 = mybir.dt.uint8
+FP8X4 = mybir.dt.float8_e4m3fn_x4
+ALU = mybir.AluOpType
+ACT = mybir.ActivationFunctionType
+
+P = 128
+PACK = 4
+K_PASS = P * PACK
+WORDS = K_PASS // 2
+PASSES = 4
+ROWS = 4096
+H = 512
+H_TILES = H // P
+EPS = 0.0001
+
+STEP_TILES = 2
+CHUNK_TILES = 4
+CHUNK_STEPS = CHUNK_TILES // STEP_TILES
+CHUNKS = ROWS // (P * CHUNK_TILES)
+STEPS = CHUNKS * CHUNK_STEPS
+CHUNKS_AHEAD = 2
+
+FLOPS = 2 * ROWS * PASSES * K_PASS * H
+
+
+def as_words(tile_2d, row_tiles):
+    return tile_2d[:].bitcast(F32).rearrange("p (t w) -> p t w", t=row_tiles)
+
+
+def passes_of_row_tile(first_words, second_words, long_words, t):
+    return [
+        first_words[:, t, :],
+        second_words[:, t, :],
+        long_words[:, t, 0:WORDS],
+        long_words[:, t, WORDS : 2 * WORDS],
+    ]
+
+
+def turn_two_passes(nc, turn_banks, identity, two_passes, grouped_words, copy_out):
+    turned = turn_banks.tile([P, 2, 2, P], F32)
+    for i in range(2):
+        for u in range(2):
+            nc.tensor.transpose(
+                out=turned[:, i, u, :],
+                in_=two_passes[i][:, u * P : (u + 1) * P],
+                identity=identity[:],
+            )
+    copy_out(out=grouped_words, in_=turned[:].rearrange("p g u r -> p g r u"))
+
+
+def tile_sparsegatedrnncell_pb_t_kernel(
+    tc, x, hx, sy, internal, W_ih, W_hh, W_sh, mu, out
+):
+    nc = tc.nc
+
+    by_chunk = "(c p t) k -> c p (t k)"
+    x_chunks = x.rearrange(by_chunk, p=P, t=CHUNK_TILES)
+    hx_chunks = hx.rearrange(by_chunk, p=P, t=CHUNK_TILES)
+    sy_chunks = sy.rearrange(by_chunk, p=P, t=CHUNK_TILES)
+    internal_chunks = internal.rearrange(by_chunk, p=P, t=CHUNK_TILES)
+    out_chunks = out.rearrange(by_chunk, p=P, t=CHUNK_TILES)
+
+    with ExitStack() as stack:
+        consts = stack.enter_context(tc.tile_pool(name="consts", bufs=1))
+        loads = stack.enter_context(tc.tile_pool(name="loads", bufs=CHUNKS_AHEAD + 1))
+        regroup = stack.enter_context(tc.tile_pool(name="regroup", bufs=2))
+        packed = stack.enter_context(tc.tile_pool(name="packed", bufs=3))
+        rowwise = stack.enter_context(tc.tile_pool(name="rowwise", bufs=3))
+        small = stack.enter_context(tc.tile_pool(name="small", bufs=4))
+        turn_banks = stack.enter_context(tc.psum_pool(name="turn_banks", bufs=4))
+        sum_banks = stack.enter_context(tc.psum_pool(name="sum_banks", bufs=4))
+
+        chunk_tiles = {}
+        step_tiles = {}
+
+        def load_chunk(c):
+            x_sb = loads.tile([P, CHUNK_TILES * K_PASS], BF16)
+            hx_sb = loads.tile([P, CHUNK_TILES * K_PASS], BF16)
+            sy_sb = loads.tile([P, CHUNK_TILES * 2 * K_PASS], BF16)
+            internal_sb = loads.tile([P, CHUNK_TILES * H], BF16)
+            nc.sync.dma_start(out=x_sb[:], in_=x_chunks[c])
+            nc.sync.dma_start(out=hx_sb[:], in_=hx_chunks[c])
+            nc.sync.dma_start(out=sy_sb[:], in_=sy_chunks[c])
+            nc.sync.dma_start(out=internal_sb[:], in_=internal_chunks[c])
+            chunk_tiles[c] = (
+                as_words(x_sb, CHUNK_TILES),
+                as_words(hx_sb, CHUNK_TILES),
+                as_words(sy_sb, CHUNK_TILES),
+                internal_sb,
+            )
+
+        by_row_tile = "(j p) k -> p j k"
+        w_ih_sb = consts.tile([P, H_TILES * K_PASS], BF16)
+        w_hh_sb = consts.tile([P, H_TILES * K_PASS], BF16)
+        w_sh_sb = consts.tile([P, H_TILES * 2 * K_PASS], BF16)
+        for w_sb, w_dram in ((w_ih_sb, W_ih), (w_hh_sb, W_hh), (w_sh_sb, W_sh)):
+            nc.sync.dma_start(
+                out=w_sb[:].rearrange("p (j k) -> p j k", j=H_TILES),
+                in_=w_dram.rearrange(by_row_tile, p=P),
+            )
+        for c in range(CHUNKS_AHEAD):
+            load_chunk(c)
+
+        identity = consts.tile([P, P], F32)
+        make_identity(nc, identity[:])
+
+        table_seed = consts.tile([P, 1], F32)
+        nc.vector.memset(table_seed[:], 1.0)
+        nc.scalar.sqrt(out=table_seed[:], in_=table_seed[:])
+
+        mu_row = consts.tile([P, H], BF16)
+        nc.vector.memset(mu_row[:], 0.0)
+        nc.sync.dma_start(out=mu_row[0:1, :], in_=mu.rearrange("(o h) -> o h", o=1))
+        ones = consts.tile([P, P], BF16)
+        nc.vector.memset(ones[:], 1.0)
+        mu_bank = sum_banks.tile([P, H], F32, tag="sums")
+        nc.tensor.matmul(out=mu_bank[:], lhsT=ones[:], rhs=mu_row[:], start=True, stop=True)
+        mu_all = consts.tile([P, H], F32)
+        nc.vector.tensor_copy(out=mu_all[:], in_=mu_bank[:])
+
+        w_grouped = consts.tile([P, PASSES * H * PACK], BF16, align_bytes=64)
+        w_codes = consts.tile([P, PASSES * H], U32, align_bytes=64)
+        w_scales = consts.tile([P, PASSES * H], U8, align_bytes=64)
+        w_grouped_words = w_grouped[:].bitcast(F32).rearrange(
+            "p (g j r u) -> p g j r u", g=PASSES, j=H_TILES, r=P, u=2
+        )
+        w_words = (
+            as_words(w_ih_sb, H_TILES),
+            as_words(w_hh_sb, H_TILES),
+            as_words(w_sh_sb, H_TILES),
+        )
+        for pair in range(PASSES // 2):
+            for j in range(H_TILES):
+                turn_two_passes(
+                    nc,
+                    turn_banks,
+                    identity,
+                    passes_of_row_tile(w_words[0], w_words[1], w_words[2], j)[2 * pair : 2 * pair + 2],
+                    w_grouped_words[:, 2 * pair : 2 * pair + 2, j, :, :],
+                    nc.scalar.copy if j % 2 == 0 else nc.vector.tensor_copy,
+                )
+            two_passes = slice(2 * pair * H, (2 * pair + 2) * H)
+            nc.vector.quantize_mx(
+                out=w_codes[:, two_passes].bitcast(FP8X4),
+                scales=w_scales[:, two_passes],
+                in_=w_grouped[:, 2 * pair * H * PACK : (2 * pair + 2) * H * PACK],
+            )
+
+        def turn(s):
+            c, first_tile = s // CHUNK_STEPS, (s % CHUNK_STEPS) * STEP_TILES
+            x_words, hx_words, sy_words = chunk_tiles[c][0:3]
+            grouped = regroup.tile([P, STEP_TILES * PASSES * P * PACK], BF16, align_bytes=64)
+            grouped_words = grouped[:].bitcast(F32).rearrange(
+                "p (t g r u) -> p t g r u", t=STEP_TILES, g=PASSES, r=P, u=2
+            )
+            for t in range(STEP_TILES):
+                four_passes = passes_of_row_tile(x_words, hx_words, sy_words, first_tile + t)
+                for pair in range(PASSES // 2):
+                    turn_two_passes(
+                        nc,
+                        turn_banks,
+                        identity,
+                        four_passes[2 * pair : 2 * pair + 2],
+                        grouped_words[:, t, 2 * pair : 2 * pair + 2, :, :],
+                        nc.scalar.copy,
+                    )
+            step_tiles[s] = {"grouped": grouped}
+
+        def quantise(s):
+            codes = packed.tile([P, STEP_TILES * PASSES * P], U32, align_bytes=64)
+            scales = packed.tile([P, STEP_TILES * PASSES * P], U8, align_bytes=64)
+            nc.vector.quantize_mx(
+                out=codes[:].bitcast(FP8X4), scales=scales[:], in_=step_tiles[s]["grouped"][:]
+            )
+            step_tiles[s]["codes"] = codes
+            step_tiles[s]["scales"] = scales
+
+        def multiply(s):
+            codes, scales = step_tiles[s]["codes"], step_tiles[s]["scales"]
+            banks = []
+            for t in range(STEP_TILES):
+                sums = sum_banks.tile([P, H], F32, tag="sums")
+                for g in range(PASSES):
+                    rows = slice((t * PASSES + g) * P, (t * PASSES + g + 1) * P)
+                    cols = slice(g * H, (g + 1) * H)
+                    nc.tensor.matmul_mx(
+                        out=sums[:],
+                        lhsT=codes[:, rows].bitcast(FP8X4),
+                        lhsT_scale=scales[:, rows],
+                        rhs=w_codes[:, cols].bitcast(FP8X4),
+                        rhs_scale=w_scales[:, cols],
+                        start=(g == 0),
+                        stop=(g == PASSES - 1),
+                    )
+                banks.append(sums)
+            step_tiles[s]["sums"] = banks
+
+        def add_mu_to_internal(s):
+            c, first_tile = s // CHUNK_STEPS, (s % CHUNK_STEPS) * STEP_TILES
+            internal_sb = chunk_tiles[c][3]
+            drive = rowwise.tile([P, STEP_TILES, H], F32)
+            for t in range(STEP_TILES):
+                nc.gpsimd.tensor_tensor(
+                    out=drive[:, t, :],
+                    in0=internal_sb[:, (first_tile + t) * H : (first_tile + t + 1) * H],
+                    in1=mu_all[:],
+                    op=ALU.add,
+                )
+            step_tiles[s]["drive"] = drive
+
+        def statistics(s):
+            stats = small.tile([P, STEP_TILES, 6], F32)
+            mean_var = small.tile([P, STEP_TILES, 2], F32)
+            for t in range(STEP_TILES):
+                nc.vector.bn_stats(out=stats[:, t, :], in_=step_tiles[s]["sums"][t][:])
+            for t in range(STEP_TILES):
+                nc.vector.bn_aggr(out=mean_var[:, t, :], in_=stats[:, t, :])
+            std = small.tile([P, STEP_TILES], F32)
+            nc.scalar.sqrt(out=std[:], in_=mean_var[:, :, 1])
+            step_tiles[s]["mean_var"] = mean_var
+            step_tiles[s]["std"] = std
+
+        def normalise(s):
+            c, step_in_chunk = s // CHUNK_STEPS, s % CHUNK_STEPS
+            mean_var, std = step_tiles[s]["mean_var"], step_tiles[s]["std"]
+            inv_std = small.tile([P, STEP_TILES], F32)
+            shift = small.tile([P, STEP_TILES], F32)
+            nc.vector.tensor_scalar_add(out=inv_std[:], in0=std[:], scalar1=EPS)
+            nc.vector.reciprocal(out=inv_std[:], in_=inv_std[:])
+            nc.vector.scalar_tensor_tensor(
+                out=shift[:], in0=mean_var[:, :, 0], scalar=-1.0, in1=inv_std[:],
+                op0=ALU.mult, op1=ALU.mult,
+            )
+            hy = rowwise.tile([P, STEP_TILES, H], F32)
+            for t in range(STEP_TILES):
+                nc.vector.scalar_tensor_tensor(
+                    out=hy[:, t, :],
+                    in0=step_tiles[s]["sums"][t][:],
+                    scalar=inv_std[:, t : t + 1],
+                    in1=step_tiles[s]["drive"][:, t, :],
+                    op0=ALU.mult,
+                    op1=ALU.add,
+                )
+                nc.scalar.activation(
+                    out=hy[:, t, :], in_=hy[:, t, :], func=ACT.Relu, bias=shift[:, t : t + 1], scale=1.0
+                )
+            nc.scalar.dma_start(
+                out=out_chunks[c][:, step_in_chunk * STEP_TILES * H : (step_in_chunk + 1) * STEP_TILES * H],
+                in_=hy[:].rearrange("p t h -> p (t h)"),
+            )
+
+        turn(0)
+        quantise(0)
+        for s in range(STEPS):
+            if s % CHUNK_STEPS == 0 and s // CHUNK_STEPS + CHUNKS_AHEAD < CHUNKS:
+                load_chunk(s // CHUNK_STEPS + CHUNKS_AHEAD)
+            if s + 1 < STEPS:
+                turn(s + 1)
+            multiply(s)
+            add_mu_to_internal(s)
+            statistics(s)
+            if s + 1 < STEPS:
+                quantise(s + 1)
+            normalise(s)

@@ -69,6 +69,7 @@ def tile_sparsegatedrnncell_pb_t_kernel(
     out_chunks = out.rearrange(by_chunk, p=P, t=CHUNK_TILES)
 
     with ExitStack() as stack:
+        stack.enter_context(tc.manual_schedule())
         consts = stack.enter_context(tc.tile_pool(name="consts", bufs=1))
         loads = stack.enter_context(tc.tile_pool(name="loads", bufs=CHUNKS_AHEAD + 1))
         regroup = stack.enter_context(tc.tile_pool(name="regroup", bufs=2))
@@ -118,7 +119,7 @@ def tile_sparsegatedrnncell_pb_t_kernel(
 
         mu_row = consts.tile([P, H], BF16)
         nc.vector.memset(mu_row[:], 0.0)
-        nc.sync.dma_start(out=mu_row[0:1, :], in_=mu.rearrange("(o h) -> o h", o=1))
+        nc.scalar.dma_start(out=mu_row[0:1, :], in_=mu.rearrange("(o h) -> o h", o=1))
         ones = consts.tile([P, P], BF16)
         nc.vector.memset(ones[:], 1.0)
         mu_bank = sum_banks.tile([P, H], F32, tag="sums")
@@ -154,25 +155,25 @@ def tile_sparsegatedrnncell_pb_t_kernel(
                 in_=w_grouped[:, 2 * pair * H * PACK : (2 * pair + 2) * H * PACK],
             )
 
-        def turn(s):
-            c, first_tile = s // CHUNK_STEPS, (s % CHUNK_STEPS) * STEP_TILES
+        def turn(s, t):
+            c, tile_in_chunk = s // CHUNK_STEPS, (s % CHUNK_STEPS) * STEP_TILES + t
             x_words, hx_words, sy_words = chunk_tiles[c][0:3]
-            grouped = regroup.tile([P, STEP_TILES * PASSES * P * PACK], BF16, align_bytes=64)
-            grouped_words = grouped[:].bitcast(F32).rearrange(
+            if t == 0:
+                grouped = regroup.tile([P, STEP_TILES * PASSES * P * PACK], BF16, align_bytes=64)
+                step_tiles[s] = {"grouped": grouped}
+            grouped_words = step_tiles[s]["grouped"][:].bitcast(F32).rearrange(
                 "p (t g r u) -> p t g r u", t=STEP_TILES, g=PASSES, r=P, u=2
             )
-            for t in range(STEP_TILES):
-                four_passes = passes_of_row_tile(x_words, hx_words, sy_words, first_tile + t)
-                for pair in range(PASSES // 2):
-                    turn_two_passes(
-                        nc,
-                        turn_banks,
-                        identity,
-                        four_passes[2 * pair : 2 * pair + 2],
-                        grouped_words[:, t, 2 * pair : 2 * pair + 2, :, :],
-                        nc.scalar.copy,
-                    )
-            step_tiles[s] = {"grouped": grouped}
+            four_passes = passes_of_row_tile(x_words, hx_words, sy_words, tile_in_chunk)
+            for pair in range(PASSES // 2):
+                turn_two_passes(
+                    nc,
+                    turn_banks,
+                    identity,
+                    four_passes[2 * pair : 2 * pair + 2],
+                    grouped_words[:, t, 2 * pair : 2 * pair + 2, :, :],
+                    nc.scalar.copy,
+                )
 
         def quantise(s):
             codes = packed.tile([P, STEP_TILES * PASSES * P], U32, align_bytes=64)
@@ -201,7 +202,9 @@ def tile_sparsegatedrnncell_pb_t_kernel(
                         stop=(g == PASSES - 1),
                     )
                 banks.append(sums)
+            stats = small.tile([P, STEP_TILES, 6], F32)
             step_tiles[s]["sums"] = banks
+            step_tiles[s]["stats"] = stats
 
         def add_mu_to_internal(s):
             c, first_tile = s // CHUNK_STEPS, (s % CHUNK_STEPS) * STEP_TILES
@@ -216,16 +219,18 @@ def tile_sparsegatedrnncell_pb_t_kernel(
                 )
             step_tiles[s]["drive"] = drive
 
-        def statistics(s):
-            stats = small.tile([P, STEP_TILES, 6], F32)
+        def row_statistics(s, t):
+            nc.vector.bn_stats(out=step_tiles[s]["stats"][:, t, :], in_=step_tiles[s]["sums"][t][:])
+
+        def mean_and_variance(s):
             mean_var = small.tile([P, STEP_TILES, 2], F32)
             for t in range(STEP_TILES):
-                nc.vector.bn_stats(out=stats[:, t, :], in_=step_tiles[s]["sums"][t][:])
-            for t in range(STEP_TILES):
-                nc.vector.bn_aggr(out=mean_var[:, t, :], in_=stats[:, t, :])
-            std = small.tile([P, STEP_TILES], F32)
-            nc.scalar.sqrt(out=std[:], in_=mean_var[:, :, 1])
+                nc.vector.bn_aggr(out=mean_var[:, t, :], in_=step_tiles[s]["stats"][:, t, :])
             step_tiles[s]["mean_var"] = mean_var
+
+        def standard_deviation(s):
+            std = small.tile([P, STEP_TILES], F32)
+            nc.scalar.sqrt(out=std[:], in_=step_tiles[s]["mean_var"][:, :, 1])
             step_tiles[s]["std"] = std
 
         def normalise(s):
@@ -257,16 +262,25 @@ def tile_sparsegatedrnncell_pb_t_kernel(
                 in_=hy[:].rearrange("p t h -> p (t h)"),
             )
 
-        turn(0)
+        for t in range(STEP_TILES):
+            turn(0, t)
         quantise(0)
-        for s in range(STEPS):
-            if s % CHUNK_STEPS == 0 and s // CHUNK_STEPS + CHUNKS_AHEAD < CHUNKS:
-                load_chunk(s // CHUNK_STEPS + CHUNKS_AHEAD)
-            if s + 1 < STEPS:
-                turn(s + 1)
-            multiply(s)
-            add_mu_to_internal(s)
-            statistics(s)
-            if s + 1 < STEPS:
-                quantise(s + 1)
-            normalise(s)
+        for k in range(STEPS + 1):
+            if k % CHUNK_STEPS == 0 and k // CHUNK_STEPS + CHUNKS_AHEAD < CHUNKS:
+                load_chunk(k // CHUNK_STEPS + CHUNKS_AHEAD)
+            if k + 1 < STEPS:
+                turn(k + 1, 0)
+            if k >= 1:
+                standard_deviation(k - 1)
+            if k + 1 < STEPS:
+                turn(k + 1, 1)
+            if k >= 1:
+                normalise(k - 1)
+            if k < STEPS:
+                add_mu_to_internal(k)
+                multiply(k)
+                row_statistics(k, 0)
+                if k + 1 < STEPS:
+                    quantise(k + 1)
+                row_statistics(k, 1)
+                mean_and_variance(k)

@@ -211,7 +211,7 @@ def tile_sparsegatedrnncell_pb_t_kernel(
             internal_sb = chunk_tiles[c][3]
             drive = rowwise.tile([P, STEP_TILES, H], F32)
             for t in range(STEP_TILES):
-                nc.gpsimd.tensor_tensor(
+                nc.vector.tensor_tensor(
                     out=drive[:, t, :],
                     in0=internal_sb[:, (first_tile + t) * H : (first_tile + t + 1) * H],
                     in1=mu_all[:],

@@ -9,7 +9,6 @@ U32 = mybir.dt.uint32
 U8 = mybir.dt.uint8
 FP8X4 = mybir.dt.float8_e4m3fn_x4
 ALU = mybir.AluOpType
-ACT = mybir.ActivationFunctionType
 
 P = 128
 PACK = 4
@@ -211,7 +210,7 @@ def tile_sparsegatedrnncell_pb_t_kernel(
             internal_sb = chunk_tiles[c][3]
             drive = rowwise.tile([P, STEP_TILES, H], F32)
             for t in range(STEP_TILES):
-                nc.vector.tensor_tensor(
+                nc.gpsimd.tensor_tensor(
                     out=drive[:, t, :],
                     in0=internal_sb[:, (first_tile + t) * H : (first_tile + t + 1) * H],
                     in1=mu_all[:],
@@ -254,10 +253,16 @@ def tile_sparsegatedrnncell_pb_t_kernel(
                     op0=ALU.mult,
                     op1=ALU.add,
                 )
-                nc.scalar.activation(
-                    out=hy[:, t, :], in_=hy[:, t, :], func=ACT.Relu, bias=shift[:, t : t + 1], scale=1.0
+            for t in range(STEP_TILES):
+                nc.vector.tensor_scalar(
+                    out=hy[:, t, :],
+                    in0=hy[:, t, :],
+                    scalar1=shift[:, t : t + 1],
+                    scalar2=0.0,
+                    op0=ALU.add,
+                    op1=ALU.max,
                 )
-            nc.scalar.dma_start(
+            nc.sync.dma_start(
                 out=out_chunks[c][:, step_in_chunk * STEP_TILES * H : (step_in_chunk + 1) * STEP_TILES * H],
                 in_=hy[:].rearrange("p t h -> p (t h)"),
             )

@@ -9,6 +9,7 @@ U32 = mybir.dt.uint32
 U8 = mybir.dt.uint8
 FP8X4 = mybir.dt.float8_e4m3fn_x4
 ALU = mybir.AluOpType
+ACT = mybir.ActivationFunctionType
 
 P = 128
 PACK = 4
@@ -18,14 +19,12 @@ PASSES = 4
 ROWS = 4096
 H = 512
 H_TILES = H // P
+TILE_WORDS = PASSES * P
 EPS = 0.0001
 
 STEP_TILES = 2
-CHUNK_TILES = 4
-CHUNK_STEPS = CHUNK_TILES // STEP_TILES
-CHUNKS = ROWS // (P * CHUNK_TILES)
-STEPS = CHUNKS * CHUNK_STEPS
-CHUNKS_AHEAD = 2
+STEPS = ROWS // (P * STEP_TILES)
+STEPS_AHEAD = 5
 
 FLOPS = 2 * ROWS * PASSES * K_PASS * H
 
@@ -60,54 +59,55 @@ def tile_sparsegatedrnncell_pb_t_kernel(
 ):
     nc = tc.nc
 
-    by_chunk = "(c p t) k -> c p (t k)"
-    x_chunks = x.rearrange(by_chunk, p=P, t=CHUNK_TILES)
-    hx_chunks = hx.rearrange(by_chunk, p=P, t=CHUNK_TILES)
-    sy_chunks = sy.rearrange(by_chunk, p=P, t=CHUNK_TILES)
-    internal_chunks = internal.rearrange(by_chunk, p=P, t=CHUNK_TILES)
-    out_chunks = out.rearrange(by_chunk, p=P, t=CHUNK_TILES)
+    by_step = "(s p t) k -> s p (t k)"
+    x_steps = x.rearrange(by_step, p=P, t=STEP_TILES)
+    hx_steps = hx.rearrange(by_step, p=P, t=STEP_TILES)
+    sy_steps = sy.rearrange(by_step, p=P, t=STEP_TILES)
+    internal_steps = internal.rearrange(by_step, p=P, t=STEP_TILES)
+    out_steps = out.rearrange(by_step, p=P, t=STEP_TILES)
 
     with ExitStack() as stack:
         stack.enter_context(tc.manual_schedule())
         consts = stack.enter_context(tc.tile_pool(name="consts", bufs=1))
-        loads = stack.enter_context(tc.tile_pool(name="loads", bufs=CHUNKS_AHEAD + 1))
+        loads = stack.enter_context(tc.tile_pool(name="loads", bufs=STEPS_AHEAD + 1))
         regroup = stack.enter_context(tc.tile_pool(name="regroup", bufs=2))
         packed = stack.enter_context(tc.tile_pool(name="packed", bufs=3))
-        rowwise = stack.enter_context(tc.tile_pool(name="rowwise", bufs=3))
+        drives = stack.enter_context(tc.tile_pool(name="drives", bufs=3 * STEP_TILES))
+        results = stack.enter_context(tc.tile_pool(name="results", bufs=3))
         small = stack.enter_context(tc.tile_pool(name="small", bufs=4))
         turn_banks = stack.enter_context(tc.psum_pool(name="turn_banks", bufs=4))
         sum_banks = stack.enter_context(tc.psum_pool(name="sum_banks", bufs=4))
 
-        chunk_tiles = {}
         step_tiles = {}
 
-        def load_chunk(c):
-            x_sb = loads.tile([P, CHUNK_TILES * K_PASS], BF16)
-            hx_sb = loads.tile([P, CHUNK_TILES * K_PASS], BF16)
-            sy_sb = loads.tile([P, CHUNK_TILES * 2 * K_PASS], BF16)
-            internal_sb = loads.tile([P, CHUNK_TILES * H], BF16)
-            nc.sync.dma_start(out=x_sb[:], in_=x_chunks[c])
-            nc.sync.dma_start(out=hx_sb[:], in_=hx_chunks[c])
-            nc.sync.dma_start(out=sy_sb[:], in_=sy_chunks[c])
-            nc.sync.dma_start(out=internal_sb[:], in_=internal_chunks[c])
-            chunk_tiles[c] = (
-                as_words(x_sb, CHUNK_TILES),
-                as_words(hx_sb, CHUNK_TILES),
-                as_words(sy_sb, CHUNK_TILES),
-                internal_sb,
-            )
+        def load_step(s):
+            x_sb = loads.tile([P, STEP_TILES * K_PASS], BF16)
+            hx_sb = loads.tile([P, STEP_TILES * K_PASS], BF16)
+            sy_sb = loads.tile([P, STEP_TILES * 2 * K_PASS], BF16)
+            internal_sb = loads.tile([P, STEP_TILES * H], BF16)
+            nc.sync.dma_start(out=x_sb[:], in_=x_steps[s])
+            nc.sync.dma_start(out=hx_sb[:], in_=hx_steps[s])
+            nc.sync.dma_start(out=sy_sb[:], in_=sy_steps[s])
+            nc.sync.dma_start(out=internal_sb[:], in_=internal_steps[s])
+            step_tiles[s] = {
+                "words": (
+                    as_words(x_sb, STEP_TILES),
+                    as_words(hx_sb, STEP_TILES),
+                    as_words(sy_sb, STEP_TILES),
+                ),
+                "internal": internal_sb,
+            }
 
-        by_row_tile = "(j p) k -> p j k"
         w_ih_sb = consts.tile([P, H_TILES * K_PASS], BF16)
         w_hh_sb = consts.tile([P, H_TILES * K_PASS], BF16)
         w_sh_sb = consts.tile([P, H_TILES * 2 * K_PASS], BF16)
         for w_sb, w_dram in ((w_ih_sb, W_ih), (w_hh_sb, W_hh), (w_sh_sb, W_sh)):
             nc.sync.dma_start(
                 out=w_sb[:].rearrange("p (j k) -> p j k", j=H_TILES),
-                in_=w_dram.rearrange(by_row_tile, p=P),
+                in_=w_dram.rearrange("(j p) k -> p j k", p=P),
             )
-        for c in range(CHUNKS_AHEAD):
-            load_chunk(c)
+        for s in range(STEPS_AHEAD):
+            load_step(s)
 
         identity = consts.tile([P, P], F32)
         make_identity(nc, identity[:])
@@ -155,15 +155,18 @@ def tile_sparsegatedrnncell_pb_t_kernel(
             )
 
         def turn(s, t):
-            c, tile_in_chunk = s // CHUNK_STEPS, (s % CHUNK_STEPS) * STEP_TILES + t
-            x_words, hx_words, sy_words = chunk_tiles[c][0:3]
             if t == 0:
-                grouped = regroup.tile([P, STEP_TILES * PASSES * P * PACK], BF16, align_bytes=64)
-                step_tiles[s] = {"grouped": grouped}
+                grouped = regroup.tile([P, STEP_TILES * TILE_WORDS * PACK], BF16, align_bytes=64)
+                codes = packed.tile([P, STEP_TILES * TILE_WORDS], U32, align_bytes=64)
+                scales = packed.tile([P, STEP_TILES * TILE_WORDS], U8, align_bytes=64)
+                step_tiles[s]["grouped"] = grouped
+                step_tiles[s]["codes"] = codes
+                step_tiles[s]["scales"] = scales
             grouped_words = step_tiles[s]["grouped"][:].bitcast(F32).rearrange(
                 "p (t g r u) -> p t g r u", t=STEP_TILES, g=PASSES, r=P, u=2
             )
-            four_passes = passes_of_row_tile(x_words, hx_words, sy_words, tile_in_chunk)
+            x_words, hx_words, sy_words = step_tiles[s]["words"]
+            four_passes = passes_of_row_tile(x_words, hx_words, sy_words, t)
             for pair in range(PASSES // 2):
                 turn_two_passes(
                     nc,
@@ -174,14 +177,13 @@ def tile_sparsegatedrnncell_pb_t_kernel(
                     nc.scalar.copy,
                 )
 
-        def quantise(s):
-            codes = packed.tile([P, STEP_TILES * PASSES * P], U32, align_bytes=64)
-            scales = packed.tile([P, STEP_TILES * PASSES * P], U8, align_bytes=64)
+        def quantise(s, t):
+            words = slice(t * TILE_WORDS, (t + 1) * TILE_WORDS)
             nc.vector.quantize_mx(
-                out=codes[:].bitcast(FP8X4), scales=scales[:], in_=step_tiles[s]["grouped"][:]
+                out=step_tiles[s]["codes"][:, words].bitcast(FP8X4),
+                scales=step_tiles[s]["scales"][:, words],
+                in_=step_tiles[s]["grouped"][:, t * TILE_WORDS * PACK : (t + 1) * TILE_WORDS * PACK],
             )
-            step_tiles[s]["codes"] = codes
-            step_tiles[s]["scales"] = scales
 
         def multiply(s):
             codes, scales = step_tiles[s]["codes"], step_tiles[s]["scales"]
@@ -201,30 +203,27 @@ def tile_sparsegatedrnncell_pb_t_kernel(
                         stop=(g == PASSES - 1),
                     )
                 banks.append(sums)
-            stats = small.tile([P, STEP_TILES, 6], F32)
             step_tiles[s]["sums"] = banks
-            step_tiles[s]["stats"] = stats
 
         def add_mu_to_internal(s):
-            c, first_tile = s // CHUNK_STEPS, (s % CHUNK_STEPS) * STEP_TILES
-            internal_sb = chunk_tiles[c][3]
-            drive = rowwise.tile([P, STEP_TILES, H], F32)
+            step_tiles[s]["drive"] = []
             for t in range(STEP_TILES):
+                drive = drives.tile([P, H], F32)
                 nc.gpsimd.tensor_tensor(
-                    out=drive[:, t, :],
-                    in0=internal_sb[:, (first_tile + t) * H : (first_tile + t + 1) * H],
+                    out=drive[:],
+                    in0=step_tiles[s]["internal"][:, t * H : (t + 1) * H],
                     in1=mu_all[:],
                     op=ALU.add,
                 )
-            step_tiles[s]["drive"] = drive
-
-        def row_statistics(s, t):
-            nc.vector.bn_stats(out=step_tiles[s]["stats"][:, t, :], in_=step_tiles[s]["sums"][t][:])
+                step_tiles[s]["drive"].append(drive)
 
         def mean_and_variance(s):
+            stats = small.tile([P, STEP_TILES, 6], F32)
             mean_var = small.tile([P, STEP_TILES, 2], F32)
             for t in range(STEP_TILES):
-                nc.vector.bn_aggr(out=mean_var[:, t, :], in_=step_tiles[s]["stats"][:, t, :])
+                nc.vector.bn_stats(out=stats[:, t, :], in_=step_tiles[s]["sums"][t][:])
+            for t in range(STEP_TILES):
+                nc.vector.bn_aggr(out=mean_var[:, t, :], in_=stats[:, t, :])
             step_tiles[s]["mean_var"] = mean_var
 
         def standard_deviation(s):
@@ -233,59 +232,50 @@ def tile_sparsegatedrnncell_pb_t_kernel(
             step_tiles[s]["std"] = std
 
         def normalise(s):
-            c, step_in_chunk = s // CHUNK_STEPS, s % CHUNK_STEPS
             mean_var, std = step_tiles[s]["mean_var"], step_tiles[s]["std"]
             inv_std = small.tile([P, STEP_TILES], F32)
             shift = small.tile([P, STEP_TILES], F32)
+            hy = results.tile([P, STEP_TILES, H], F32)
             nc.vector.tensor_scalar_add(out=inv_std[:], in0=std[:], scalar1=EPS)
             nc.vector.reciprocal(out=inv_std[:], in_=inv_std[:])
-            nc.vector.scalar_tensor_tensor(
-                out=shift[:], in0=mean_var[:, :, 0], scalar=-1.0, in1=inv_std[:],
-                op0=ALU.mult, op1=ALU.mult,
-            )
-            hy = rowwise.tile([P, STEP_TILES, H], F32)
             for t in range(STEP_TILES):
                 nc.vector.scalar_tensor_tensor(
                     out=hy[:, t, :],
                     in0=step_tiles[s]["sums"][t][:],
                     scalar=inv_std[:, t : t + 1],
-                    in1=step_tiles[s]["drive"][:, t, :],
+                    in1=step_tiles[s]["drive"][t][:],
                     op0=ALU.mult,
                     op1=ALU.add,
                 )
+                if t == 0:
+                    nc.vector.scalar_tensor_tensor(
+                        out=shift[:], in0=mean_var[:, :, 0], scalar=-1.0, in1=inv_std[:],
+                        op0=ALU.mult, op1=ALU.mult,
+                    )
             for t in range(STEP_TILES):
-                nc.vector.tensor_scalar(
-                    out=hy[:, t, :],
-                    in0=hy[:, t, :],
-                    scalar1=shift[:, t : t + 1],
-                    scalar2=0.0,
-                    op0=ALU.add,
-                    op1=ALU.max,
+                nc.scalar.activation(
+                    out=hy[:, t, :], in_=hy[:, t, :], func=ACT.Relu, bias=shift[:, t : t + 1], scale=1.0
                 )
-            nc.sync.dma_start(
-                out=out_chunks[c][:, step_in_chunk * STEP_TILES * H : (step_in_chunk + 1) * STEP_TILES * H],
-                in_=hy[:].rearrange("p t h -> p (t h)"),
-            )
+            nc.scalar.dma_start(out=out_steps[s], in_=hy[:].rearrange("p t h -> p (t h)"))
 
+        for s in range(2):
+            for t in range(STEP_TILES):
+                turn(s, t)
         for t in range(STEP_TILES):
-            turn(0, t)
-        quantise(0)
-        for k in range(STEPS + 1):
-            if k % CHUNK_STEPS == 0 and k // CHUNK_STEPS + CHUNKS_AHEAD < CHUNKS:
-                load_chunk(k // CHUNK_STEPS + CHUNKS_AHEAD)
+            quantise(0, t)
+        for k in range(STEPS):
+            if k + STEPS_AHEAD < STEPS:
+                load_step(k + STEPS_AHEAD)
+            add_mu_to_internal(k)
+            multiply(k)
             if k + 1 < STEPS:
-                turn(k + 1, 0)
-            if k >= 1:
-                standard_deviation(k - 1)
+                quantise(k + 1, 0)
+            if k + 2 < STEPS:
+                turn(k + 2, 0)
+            mean_and_variance(k)
+            standard_deviation(k)
+            if k + 2 < STEPS:
+                turn(k + 2, 1)
             if k + 1 < STEPS:
-                turn(k + 1, 1)
-            if k >= 1:
-                normalise(k - 1)
-            if k < STEPS:
-                add_mu_to_internal(k)
-                multiply(k)
-                row_statistics(k, 0)
-                if k + 1 < STEPS:
-                    quantise(k + 1)
-                row_statistics(k, 1)
-                mean_and_variance(k)
+                quantise(k + 1, 1)
+            normalise(k)

@@ -24,6 +24,7 @@ EPS = 0.0001
 
 STEP_TILES = 2
 STEPS = ROWS // (P * STEP_TILES)
+BANKS = STEP_TILES * PASSES // 2
 STEPS_AHEAD = 5
 
 FLOPS = 2 * ROWS * PASSES * K_PASS * H
@@ -121,10 +122,6 @@ def tile_sparsegatedrnncell_pb_t_kernel(
         nc.scalar.dma_start(out=mu_row[0:1, :], in_=mu.rearrange("(o h) -> o h", o=1))
         ones = consts.tile([P, P], BF16)
         nc.vector.memset(ones[:], 1.0)
-        mu_bank = sum_banks.tile([P, H], F32, tag="sums")
-        nc.tensor.matmul(out=mu_bank[:], lhsT=ones[:], rhs=mu_row[:], start=True, stop=True)
-        mu_all = consts.tile([P, H], F32)
-        nc.vector.tensor_copy(out=mu_all[:], in_=mu_bank[:])
 
         w_grouped = consts.tile([P, PASSES * H * PACK], BF16, align_bytes=64)
         w_codes = consts.tile([P, PASSES * H], U32, align_bytes=64)
@@ -154,8 +151,14 @@ def tile_sparsegatedrnncell_pb_t_kernel(
                 in_=w_grouped[:, 2 * pair * H * PACK : (2 * pair + 2) * H * PACK],
             )
 
-        def turn(s, t):
-            if t == 0:
+        mu_bank = sum_banks.tile([P, H], F32, tag="sums")
+        nc.tensor.matmul(out=mu_bank[:], lhsT=ones[:], rhs=mu_row[:], start=True, stop=True)
+        mu_all = consts.tile([P, H], F32)
+        nc.vector.tensor_copy(out=mu_all[:], in_=mu_bank[:])
+
+        def turn(s, bank):
+            t, pair = bank // 2, bank % 2
+            if bank == 0:
                 grouped = regroup.tile([P, STEP_TILES * TILE_WORDS * PACK], BF16, align_bytes=64)
                 codes = packed.tile([P, STEP_TILES * TILE_WORDS], U32, align_bytes=64)
                 scales = packed.tile([P, STEP_TILES * TILE_WORDS], U8, align_bytes=64)
@@ -166,16 +169,14 @@ def tile_sparsegatedrnncell_pb_t_kernel(
                 "p (t g r u) -> p t g r u", t=STEP_TILES, g=PASSES, r=P, u=2
             )
             x_words, hx_words, sy_words = step_tiles[s]["words"]
-            four_passes = passes_of_row_tile(x_words, hx_words, sy_words, t)
-            for pair in range(PASSES // 2):
-                turn_two_passes(
-                    nc,
-                    turn_banks,
-                    identity,
-                    four_passes[2 * pair : 2 * pair + 2],
-                    grouped_words[:, t, 2 * pair : 2 * pair + 2, :, :],
-                    nc.scalar.copy,
-                )
+            turn_two_passes(
+                nc,
+                turn_banks,
+                identity,
+                passes_of_row_tile(x_words, hx_words, sy_words, t)[2 * pair : 2 * pair + 2],
+                grouped_words[:, t, 2 * pair : 2 * pair + 2, :, :],
+                nc.scalar.copy,
+            )
 
         def quantise(s, t):
             words = slice(t * TILE_WORDS, (t + 1) * TILE_WORDS)
@@ -231,13 +232,17 @@ def tile_sparsegatedrnncell_pb_t_kernel(
             nc.scalar.sqrt(out=std[:], in_=step_tiles[s]["mean_var"][:, :, 1])
             step_tiles[s]["std"] = std
 
+        def add_eps(s):
+            std_eps = small.tile([P, STEP_TILES], F32)
+            nc.vector.tensor_scalar_add(out=std_eps[:], in0=step_tiles[s]["std"][:], scalar1=EPS)
+            step_tiles[s]["std_eps"] = std_eps
+
         def normalise(s):
-            mean_var, std = step_tiles[s]["mean_var"], step_tiles[s]["std"]
+            mean_var = step_tiles[s]["mean_var"]
             inv_std = small.tile([P, STEP_TILES], F32)
             shift = small.tile([P, STEP_TILES], F32)
             hy = results.tile([P, STEP_TILES, H], F32)
-            nc.vector.tensor_scalar_add(out=inv_std[:], in0=std[:], scalar1=EPS)
-            nc.vector.reciprocal(out=inv_std[:], in_=inv_std[:])
+            nc.vector.reciprocal(out=inv_std[:], in_=step_tiles[s]["std_eps"][:])
             for t in range(STEP_TILES):
                 nc.vector.scalar_tensor_tensor(
                     out=hy[:, t, :],
@@ -259,8 +264,8 @@ def tile_sparsegatedrnncell_pb_t_kernel(
             nc.scalar.dma_start(out=out_steps[s], in_=hy[:].rearrange("p t h -> p (t h)"))
 
         for s in range(2):
-            for t in range(STEP_TILES):
-                turn(s, t)
+            for bank in range(BANKS):
+                turn(s, bank)
         for t in range(STEP_TILES):
             quantise(0, t)
         for k in range(STEPS):
@@ -268,14 +273,16 @@ def tile_sparsegatedrnncell_pb_t_kernel(
                 load_step(k + STEPS_AHEAD)
             add_mu_to_internal(k)
             multiply(k)
-            if k + 1 < STEPS:
-                quantise(k + 1, 0)
+            mean_and_variance(k)
             if k + 2 < STEPS:
                 turn(k + 2, 0)
-            mean_and_variance(k)
             standard_deviation(k)
             if k + 2 < STEPS:
-                turn(k + 2, 1)
+                for bank in range(1, BANKS):
+                    turn(k + 2, bank)
+            if k + 1 < STEPS:
+                quantise(k + 1, 0)
+            add_eps(k)
             if k + 1 < STEPS:
                 quantise(k + 1, 1)
             normalise(k)

@@ -24,7 +24,6 @@ EPS = 0.0001
 
 STEP_TILES = 2
 STEPS = ROWS // (P * STEP_TILES)
-BANKS = STEP_TILES * PASSES // 2
 STEPS_AHEAD = 5
 
 FLOPS = 2 * ROWS * PASSES * K_PASS * H
@@ -156,9 +155,8 @@ def tile_sparsegatedrnncell_pb_t_kernel(
         mu_all = consts.tile([P, H], F32)
         nc.vector.tensor_copy(out=mu_all[:], in_=mu_bank[:])
 
-        def turn(s, bank):
-            t, pair = bank // 2, bank % 2
-            if bank == 0:
+        def turn(s, t):
+            if t == 0:
                 grouped = regroup.tile([P, STEP_TILES * TILE_WORDS * PACK], BF16, align_bytes=64)
                 codes = packed.tile([P, STEP_TILES * TILE_WORDS], U32, align_bytes=64)
                 scales = packed.tile([P, STEP_TILES * TILE_WORDS], U8, align_bytes=64)
@@ -169,14 +167,16 @@ def tile_sparsegatedrnncell_pb_t_kernel(
                 "p (t g r u) -> p t g r u", t=STEP_TILES, g=PASSES, r=P, u=2
             )
             x_words, hx_words, sy_words = step_tiles[s]["words"]
-            turn_two_passes(
-                nc,
-                turn_banks,
-                identity,
-                passes_of_row_tile(x_words, hx_words, sy_words, t)[2 * pair : 2 * pair + 2],
-                grouped_words[:, t, 2 * pair : 2 * pair + 2, :, :],
-                nc.scalar.copy,
-            )
+            four_passes = passes_of_row_tile(x_words, hx_words, sy_words, t)
+            for pair in range(PASSES // 2):
+                turn_two_passes(
+                    nc,
+                    turn_banks,
+                    identity,
+                    four_passes[2 * pair : 2 * pair + 2],
+                    grouped_words[:, t, 2 * pair : 2 * pair + 2, :, :],
+                    nc.scalar.copy,
+                )
 
         def quantise(s, t):
             words = slice(t * TILE_WORDS, (t + 1) * TILE_WORDS)
@@ -186,25 +186,24 @@ def tile_sparsegatedrnncell_pb_t_kernel(
                 in_=step_tiles[s]["grouped"][:, t * TILE_WORDS * PACK : (t + 1) * TILE_WORDS * PACK],
             )
 
-        def multiply(s):
+        def multiply(s, t):
             codes, scales = step_tiles[s]["codes"], step_tiles[s]["scales"]
-            banks = []
-            for t in range(STEP_TILES):
-                sums = sum_banks.tile([P, H], F32, tag="sums")
-                for g in range(PASSES):
-                    rows = slice((t * PASSES + g) * P, (t * PASSES + g + 1) * P)
-                    cols = slice(g * H, (g + 1) * H)
-                    nc.tensor.matmul_mx(
-                        out=sums[:],
-                        lhsT=codes[:, rows].bitcast(FP8X4),
-                        lhsT_scale=scales[:, rows],
-                        rhs=w_codes[:, cols].bitcast(FP8X4),
-                        rhs_scale=w_scales[:, cols],
-                        start=(g == 0),
-                        stop=(g == PASSES - 1),
-                    )
-                banks.append(sums)
-            step_tiles[s]["sums"] = banks
+            sums = sum_banks.tile([P, H], F32, tag="sums")
+            for g in range(PASSES):
+                rows = slice((t * PASSES + g) * P, (t * PASSES + g + 1) * P)
+                cols = slice(g * H, (g + 1) * H)
+                nc.tensor.matmul_mx(
+                    out=sums[:],
+                    lhsT=codes[:, rows].bitcast(FP8X4),
+                    lhsT_scale=scales[:, rows],
+                    rhs=w_codes[:, cols].bitcast(FP8X4),
+                    rhs_scale=w_scales[:, cols],
+                    start=(g == 0),
+                    stop=(g == PASSES - 1),
+                )
+            if t == 0:
+                step_tiles[s]["sums"] = []
+            step_tiles[s]["sums"].append(sums)
 
         def add_mu_to_internal(s):
             step_tiles[s]["drive"] = []
@@ -237,7 +236,7 @@ def tile_sparsegatedrnncell_pb_t_kernel(
             nc.vector.tensor_scalar_add(out=std_eps[:], in0=step_tiles[s]["std"][:], scalar1=EPS)
             step_tiles[s]["std_eps"] = std_eps
 
-        def normalise(s):
+        def scale_and_add(s):
             mean_var = step_tiles[s]["mean_var"]
             inv_std = small.tile([P, STEP_TILES], F32)
             shift = small.tile([P, STEP_TILES], F32)
@@ -257,32 +256,50 @@ def tile_sparsegatedrnncell_pb_t_kernel(
                         out=shift[:], in0=mean_var[:, :, 0], scalar=-1.0, in1=inv_std[:],
                         op0=ALU.mult, op1=ALU.mult,
                     )
-            for t in range(STEP_TILES):
-                nc.scalar.activation(
-                    out=hy[:, t, :], in_=hy[:, t, :], func=ACT.Relu, bias=shift[:, t : t + 1], scale=1.0
-                )
-            nc.scalar.dma_start(out=out_steps[s], in_=hy[:].rearrange("p t h -> p (t h)"))
+            step_tiles[s]["shift"] = shift
+            step_tiles[s]["hy"] = hy
+
+        def relu(s, t):
+            hy, shift = step_tiles[s]["hy"], step_tiles[s]["shift"]
+            nc.scalar.activation(
+                out=hy[:, t, :], in_=hy[:, t, :], func=ACT.Relu, bias=shift[:, t : t + 1], scale=1.0
+            )
+
+        def store(s):
+            nc.scalar.dma_start(
+                out=out_steps[s], in_=step_tiles[s]["hy"][:].rearrange("p t h -> p (t h)")
+            )
 
         for s in range(2):
-            for bank in range(BANKS):
-                turn(s, bank)
+            for t in range(STEP_TILES):
+                turn(s, t)
         for t in range(STEP_TILES):
             quantise(0, t)
-        for k in range(STEPS):
+            multiply(0, t)
+        for t in range(STEP_TILES):
+            turn(2, t)
+            quantise(1, t)
+        for k in range(STEPS + 1):
             if k + STEPS_AHEAD < STEPS:
                 load_step(k + STEPS_AHEAD)
-            add_mu_to_internal(k)
-            multiply(k)
-            mean_and_variance(k)
-            if k + 2 < STEPS:
-                turn(k + 2, 0)
-            standard_deviation(k)
-            if k + 2 < STEPS:
-                for bank in range(1, BANKS):
-                    turn(k + 2, bank)
-            if k + 1 < STEPS:
-                quantise(k + 1, 0)
-            add_eps(k)
-            if k + 1 < STEPS:
-                quantise(k + 1, 1)
-            normalise(k)
+            if k < STEPS:
+                add_mu_to_internal(k)
+                mean_and_variance(k)
+            for t in range(STEP_TILES):
+                if k + 3 < STEPS:
+                    turn(k + 3, t)
+                if t == 0 and k < STEPS:
+                    standard_deviation(k)
+                if k + 1 < STEPS:
+                    multiply(k + 1, t)
+                if k >= 1:
+                    relu(k - 1, t)
+            if k >= 1:
+                store(k - 1)
+            if k < STEPS:
+                if k + 2 < STEPS:
+                    quantise(k + 2, 0)
+                add_eps(k)
+                if k + 2 < STEPS:
+                    quantise(k + 2, 1)
+                scale_and_add(k)

@@ -232,37 +232,44 @@ def tile_sparsegatedrnncell_pb_t_kernel(
             step_tiles[s]["std"] = std
 
         def add_eps(s):
-            std_eps = small.tile([P, STEP_TILES], F32)
-            nc.vector.tensor_scalar_add(out=std_eps[:], in0=step_tiles[s]["std"][:], scalar1=EPS)
-            step_tiles[s]["std_eps"] = std_eps
+            minus_std = small.tile([P, STEP_TILES], F32)
+            nc.vector.tensor_scalar(
+                out=minus_std[:], in0=step_tiles[s]["std"][:], scalar1=-1.0, scalar2=EPS,
+                op0=ALU.mult, op1=ALU.subtract,
+            )
+            step_tiles[s]["minus_std"] = minus_std
 
         def scale_and_add(s):
-            mean_var = step_tiles[s]["mean_var"]
-            inv_std = small.tile([P, STEP_TILES], F32)
-            shift = small.tile([P, STEP_TILES], F32)
-            hy = results.tile([P, STEP_TILES, H], F32)
-            nc.vector.reciprocal(out=inv_std[:], in_=step_tiles[s]["std_eps"][:])
+            minus_inv = small.tile([P, STEP_TILES], F32)
+            minus_hy = results.tile([P, STEP_TILES, H], F32)
+            nc.vector.reciprocal(out=minus_inv[:], in_=step_tiles[s]["minus_std"][:])
             for t in range(STEP_TILES):
                 nc.vector.scalar_tensor_tensor(
-                    out=hy[:, t, :],
+                    out=minus_hy[:, t, :],
                     in0=step_tiles[s]["sums"][t][:],
-                    scalar=inv_std[:, t : t + 1],
+                    scalar=minus_inv[:, t : t + 1],
                     in1=step_tiles[s]["drive"][t][:],
                     op0=ALU.mult,
-                    op1=ALU.add,
+                    op1=ALU.subtract,
                 )
-                if t == 0:
-                    nc.vector.scalar_tensor_tensor(
-                        out=shift[:], in0=mean_var[:, :, 0], scalar=-1.0, in1=inv_std[:],
-                        op0=ALU.mult, op1=ALU.mult,
-                    )
+            step_tiles[s]["minus_inv"] = minus_inv
+            step_tiles[s]["hy"] = minus_hy
+
+        def shift_by_mean(s):
+            shift = small.tile([P, STEP_TILES], F32)
+            for t in range(STEP_TILES):
+                nc.scalar.activation(
+                    out=shift[:, t : t + 1],
+                    in_=step_tiles[s]["mean_var"][:, t, 0:1],
+                    func=ACT.Copy,
+                    scale=step_tiles[s]["minus_inv"][:, t : t + 1],
+                )
             step_tiles[s]["shift"] = shift
-            step_tiles[s]["hy"] = hy
 
         def relu(s, t):
             hy, shift = step_tiles[s]["hy"], step_tiles[s]["shift"]
             nc.scalar.activation(
-                out=hy[:, t, :], in_=hy[:, t, :], func=ACT.Relu, bias=shift[:, t : t + 1], scale=1.0
+                out=hy[:, t, :], in_=hy[:, t, :], func=ACT.Relu, bias=shift[:, t : t + 1], scale=-1.0
             )
 
         def store(s):
@@ -285,6 +292,8 @@ def tile_sparsegatedrnncell_pb_t_kernel(
             if k < STEPS:
                 add_mu_to_internal(k)
                 mean_and_variance(k)
+            if k >= 1:
+                shift_by_mean(k - 1)
             for t in range(STEP_TILES):
                 if k + 3 < STEPS:
                     turn(k + 3, t)

@@ -22,9 +22,11 @@ H_TILES = H // P
 TILE_WORDS = PASSES * P
 EPS = 0.0001
 
-STEP_TILES = 2
-STEPS = ROWS // (P * STEP_TILES)
-STEPS_AHEAD = 5
+TILES = ROWS // P
+GROUP_TILES = 4
+GROUPS = TILES // GROUP_TILES
+GROUP_BUFS = 4
+STORE_TILES = 2
 
 FLOPS = 2 * ROWS * PASSES * K_PASS * H
 
@@ -33,22 +35,13 @@ def as_words(tile_2d, row_tiles):
     return tile_2d[:].bitcast(F32).rearrange("p (t w) -> p t w", t=row_tiles)
 
 
-def passes_of_row_tile(first_words, second_words, long_words, t):
-    return [
-        first_words[:, t, :],
-        second_words[:, t, :],
-        long_words[:, t, 0:WORDS],
-        long_words[:, t, WORDS : 2 * WORDS],
-    ]
-
-
-def turn_two_passes(nc, turn_banks, identity, two_passes, grouped_words, copy_out):
+def turn_into_bank(nc, turn_banks, identity, two_sources, grouped_words, copy_out):
     turned = turn_banks.tile([P, 2, 2, P], F32)
     for i in range(2):
         for u in range(2):
             nc.tensor.transpose(
                 out=turned[:, i, u, :],
-                in_=two_passes[i][:, u * P : (u + 1) * P],
+                in_=two_sources[i][:, u * P : (u + 1) * P],
                 identity=identity[:],
             )
     copy_out(out=grouped_words, in_=turned[:].rearrange("p g u r -> p g r u"))
@@ -59,44 +52,55 @@ def tile_sparsegatedrnncell_pb_t_kernel(
 ):
     nc = tc.nc
 
-    by_step = "(s p t) k -> s p (t k)"
-    x_steps = x.rearrange(by_step, p=P, t=STEP_TILES)
-    hx_steps = hx.rearrange(by_step, p=P, t=STEP_TILES)
-    sy_steps = sy.rearrange(by_step, p=P, t=STEP_TILES)
-    internal_steps = internal.rearrange(by_step, p=P, t=STEP_TILES)
-    out_steps = out.rearrange(by_step, p=P, t=STEP_TILES)
+    by_group = "(g p t) k -> g p t k"
+    x_groups = x.rearrange(by_group, p=P, t=GROUP_TILES)
+    hx_groups = hx.rearrange(by_group, p=P, t=GROUP_TILES)
+    sy_groups = sy.rearrange(by_group, p=P, t=GROUP_TILES)
+    internal_groups = internal.rearrange(by_group, p=P, t=GROUP_TILES)
+    out_groups = out.rearrange(by_group, p=P, t=GROUP_TILES)
 
     with ExitStack() as stack:
         stack.enter_context(tc.manual_schedule())
         consts = stack.enter_context(tc.tile_pool(name="consts", bufs=1))
-        loads = stack.enter_context(tc.tile_pool(name="loads", bufs=STEPS_AHEAD + 1))
-        regroup = stack.enter_context(tc.tile_pool(name="regroup", bufs=2))
-        packed = stack.enter_context(tc.tile_pool(name="packed", bufs=3))
-        drives = stack.enter_context(tc.tile_pool(name="drives", bufs=3 * STEP_TILES))
-        results = stack.enter_context(tc.tile_pool(name="results", bufs=3))
-        small = stack.enter_context(tc.tile_pool(name="small", bufs=4))
+        loads = stack.enter_context(tc.tile_pool(name="loads", bufs=GROUP_BUFS))
+        regroup = stack.enter_context(tc.tile_pool(name="regroup", bufs=5))
+        packed = stack.enter_context(tc.tile_pool(name="packed", bufs=4))
+        results = stack.enter_context(tc.tile_pool(name="results", bufs=4))
+        small = stack.enter_context(tc.tile_pool(name="small", bufs=6))
         turn_banks = stack.enter_context(tc.psum_pool(name="turn_banks", bufs=4))
         sum_banks = stack.enter_context(tc.psum_pool(name="sum_banks", bufs=4))
 
-        step_tiles = {}
+        groups = {}
+        tiles = {}
 
-        def load_step(s):
-            x_sb = loads.tile([P, STEP_TILES * K_PASS], BF16)
-            hx_sb = loads.tile([P, STEP_TILES * K_PASS], BF16)
-            sy_sb = loads.tile([P, STEP_TILES * 2 * K_PASS], BF16)
-            internal_sb = loads.tile([P, STEP_TILES * H], BF16)
-            nc.sync.dma_start(out=x_sb[:], in_=x_steps[s])
-            nc.sync.dma_start(out=hx_sb[:], in_=hx_steps[s])
-            nc.sync.dma_start(out=sy_sb[:], in_=sy_steps[s])
-            nc.sync.dma_start(out=internal_sb[:], in_=internal_steps[s])
-            step_tiles[s] = {
-                "words": (
-                    as_words(x_sb, STEP_TILES),
-                    as_words(hx_sb, STEP_TILES),
-                    as_words(sy_sb, STEP_TILES),
-                ),
-                "internal": internal_sb,
+        def load_activations(g, parts):
+            x_sb = loads.tile([P, GROUP_TILES * K_PASS], BF16)
+            hx_sb = loads.tile([P, GROUP_TILES * K_PASS], BF16)
+            sy_sb = loads.tile([P, GROUP_TILES * 2 * K_PASS], BF16)
+            groups[g] = {
+                "x": as_words(x_sb, GROUP_TILES),
+                "hx": as_words(hx_sb, GROUP_TILES),
+                "sy": as_words(sy_sb, GROUP_TILES),
             }
+            wide = GROUP_TILES // parts
+            for part in range(parts):
+                t = slice(part * wide, (part + 1) * wide)
+                for sb, dram in ((x_sb, x_groups), (hx_sb, hx_groups), (sy_sb, sy_groups)):
+                    nc.sync.dma_start(
+                        out=sb[:].rearrange("p (t k) -> p t k", t=GROUP_TILES)[:, t, :],
+                        in_=dram[g][:, t, :],
+                    )
+
+        def load_internal(g):
+            internal_sb = loads.tile([P, GROUP_TILES, H], BF16)
+            nc.sync.dma_start(out=internal_sb[:], in_=internal_groups[g])
+            groups[g]["internal"] = internal_sb
+
+        mu_row = consts.tile([P, H], BF16)
+        nc.vector.memset(mu_row[:], 0.0)
+        nc.scalar.dma_start(out=mu_row[0:1, :], in_=mu.rearrange("(o h) -> o h", o=1))
+        ones = consts.tile([P, P], BF16)
+        nc.vector.memset(ones[:], 1.0)
 
         w_ih_sb = consts.tile([P, H_TILES * K_PASS], BF16)
         w_hh_sb = consts.tile([P, H_TILES * K_PASS], BF16)
@@ -106,8 +110,11 @@ def tile_sparsegatedrnncell_pb_t_kernel(
                 out=w_sb[:].rearrange("p (j k) -> p j k", j=H_TILES),
                 in_=w_dram.rearrange("(j p) k -> p j k", p=P),
             )
-        for s in range(STEPS_AHEAD):
-            load_step(s)
+        for g in range(GROUP_BUFS):
+            load_activations(g, 2 if g < 2 else 1)
+            if g >= 1:
+                load_internal(g - 1)
+        load_internal(GROUP_BUFS - 1)
 
         identity = consts.tile([P, P], F32)
         make_identity(nc, identity[:])
@@ -116,81 +123,78 @@ def tile_sparsegatedrnncell_pb_t_kernel(
         nc.vector.memset(table_seed[:], 1.0)
         nc.scalar.sqrt(out=table_seed[:], in_=table_seed[:])
 
-        mu_row = consts.tile([P, H], BF16)
-        nc.vector.memset(mu_row[:], 0.0)
-        nc.scalar.dma_start(out=mu_row[0:1, :], in_=mu.rearrange("(o h) -> o h", o=1))
-        ones = consts.tile([P, P], BF16)
-        nc.vector.memset(ones[:], 1.0)
-
         w_grouped = consts.tile([P, PASSES * H * PACK], BF16, align_bytes=64)
         w_codes = consts.tile([P, PASSES * H], U32, align_bytes=64)
         w_scales = consts.tile([P, PASSES * H], U8, align_bytes=64)
         w_grouped_words = w_grouped[:].bitcast(F32).rearrange(
             "p (g j r u) -> p g j r u", g=PASSES, j=H_TILES, r=P, u=2
         )
+        w_ih_words = as_words(w_ih_sb, H_TILES)
+        w_hh_words = as_words(w_hh_sb, H_TILES)
+        w_sh_words = as_words(w_sh_sb, H_TILES)
         w_words = (
-            as_words(w_ih_sb, H_TILES),
-            as_words(w_hh_sb, H_TILES),
-            as_words(w_sh_sb, H_TILES),
+            w_ih_words,
+            w_hh_words,
+            w_sh_words[:, :, 0:WORDS],
+            w_sh_words[:, :, WORDS : 2 * WORDS],
         )
-        for pair in range(PASSES // 2):
-            for j in range(H_TILES):
-                turn_two_passes(
+        for g in range(PASSES):
+            for j in range(0, H_TILES, 2):
+                turn_into_bank(
                     nc,
                     turn_banks,
                     identity,
-                    passes_of_row_tile(w_words[0], w_words[1], w_words[2], j)[2 * pair : 2 * pair + 2],
-                    w_grouped_words[:, 2 * pair : 2 * pair + 2, j, :, :],
-                    nc.scalar.copy if j % 2 == 0 else nc.vector.tensor_copy,
+                    [w_words[g][:, j, :], w_words[g][:, j + 1, :]],
+                    w_grouped_words[:, g, j : j + 2, :, :],
+                    nc.scalar.copy if j == 0 else nc.vector.tensor_copy,
                 )
-            two_passes = slice(2 * pair * H, (2 * pair + 2) * H)
+            one_pass = slice(g * H, (g + 1) * H)
             nc.vector.quantize_mx(
-                out=w_codes[:, two_passes].bitcast(FP8X4),
-                scales=w_scales[:, two_passes],
-                in_=w_grouped[:, 2 * pair * H * PACK : (2 * pair + 2) * H * PACK],
+                out=w_codes[:, one_pass].bitcast(FP8X4),
+                scales=w_scales[:, one_pass],
+                in_=w_grouped[:, g * H * PACK : (g + 1) * H * PACK],
             )
 
         mu_bank = sum_banks.tile([P, H], F32, tag="sums")
         nc.tensor.matmul(out=mu_bank[:], lhsT=ones[:], rhs=mu_row[:], start=True, stop=True)
         mu_all = consts.tile([P, H], F32)
-        nc.vector.tensor_copy(out=mu_all[:], in_=mu_bank[:])
+        nc.scalar.copy(out=mu_all[:], in_=mu_bank[:])
 
-        def turn(s, t):
-            if t == 0:
-                grouped = regroup.tile([P, STEP_TILES * TILE_WORDS * PACK], BF16, align_bytes=64)
-                codes = packed.tile([P, STEP_TILES * TILE_WORDS], U32, align_bytes=64)
-                scales = packed.tile([P, STEP_TILES * TILE_WORDS], U8, align_bytes=64)
-                step_tiles[s]["grouped"] = grouped
-                step_tiles[s]["codes"] = codes
-                step_tiles[s]["scales"] = scales
-            grouped_words = step_tiles[s]["grouped"][:].bitcast(F32).rearrange(
-                "p (t g r u) -> p t g r u", t=STEP_TILES, g=PASSES, r=P, u=2
+        def new_grouped(i):
+            grouped = regroup.tile([P, TILE_WORDS * PACK], BF16, align_bytes=64)
+            tiles[i] = {"grouped": grouped}
+
+        def turn(i, pair):
+            group, t = groups[i // GROUP_TILES], i % GROUP_TILES
+            if pair == 0:
+                two_passes = [group["x"][:, t, :], group["hx"][:, t, :]]
+            else:
+                two_passes = [group["sy"][:, t, 0:WORDS], group["sy"][:, t, WORDS : 2 * WORDS]]
+            grouped_words = tiles[i]["grouped"][:].bitcast(F32).rearrange(
+                "p (g r u) -> p g r u", g=PASSES, r=P, u=2
             )
-            x_words, hx_words, sy_words = step_tiles[s]["words"]
-            four_passes = passes_of_row_tile(x_words, hx_words, sy_words, t)
-            for pair in range(PASSES // 2):
-                turn_two_passes(
-                    nc,
-                    turn_banks,
-                    identity,
-                    four_passes[2 * pair : 2 * pair + 2],
-                    grouped_words[:, t, 2 * pair : 2 * pair + 2, :, :],
-                    nc.scalar.copy,
-                )
+            turn_into_bank(
+                nc,
+                turn_banks,
+                identity,
+                two_passes,
+                grouped_words[:, 2 * pair : 2 * pair + 2, :, :],
+                nc.scalar.copy,
+            )
 
-        def quantise(s, t):
-            words = slice(t * TILE_WORDS, (t + 1) * TILE_WORDS)
+        def quantise(i):
+            codes = packed.tile([P, TILE_WORDS], U32, align_bytes=64)
+            scales = packed.tile([P, TILE_WORDS], U8, align_bytes=64)
             nc.vector.quantize_mx(
-                out=step_tiles[s]["codes"][:, words].bitcast(FP8X4),
-                scales=step_tiles[s]["scales"][:, words],
-                in_=step_tiles[s]["grouped"][:, t * TILE_WORDS * PACK : (t + 1) * TILE_WORDS * PACK],
+                out=codes[:].bitcast(FP8X4), scales=scales[:], in_=tiles[i]["grouped"][:]
             )
+            tiles[i]["codes"], tiles[i]["scales"] = codes, scales
 
-        def multiply(s, t):
-            codes, scales = step_tiles[s]["codes"], step_tiles[s]["scales"]
+        def multiply(i):
+            codes, scales = tiles[i]["codes"], tiles[i]["scales"]
             sums = sum_banks.tile([P, H], F32, tag="sums")
             for g in range(PASSES):
-                rows = slice((t * PASSES + g) * P, (t * PASSES + g + 1) * P)
+                rows = slice(g * P, (g + 1) * P)
                 cols = slice(g * H, (g + 1) * H)
                 nc.tensor.matmul_mx(
                     out=sums[:],
@@ -201,114 +205,121 @@ def tile_sparsegatedrnncell_pb_t_kernel(
                     start=(g == 0),
                     stop=(g == PASSES - 1),
                 )
-            if t == 0:
-                step_tiles[s]["sums"] = []
-            step_tiles[s]["sums"].append(sums)
+            tiles[i]["sums"] = sums
 
-        def add_mu_to_internal(s):
-            step_tiles[s]["drive"] = []
-            for t in range(STEP_TILES):
-                drive = drives.tile([P, H], F32)
-                nc.gpsimd.tensor_tensor(
-                    out=drive[:],
-                    in0=step_tiles[s]["internal"][:, t * H : (t + 1) * H],
-                    in1=mu_all[:],
-                    op=ALU.add,
-                )
-                step_tiles[s]["drive"].append(drive)
-
-        def mean_and_variance(s):
-            stats = small.tile([P, STEP_TILES, 6], F32)
-            mean_var = small.tile([P, STEP_TILES, 2], F32)
-            for t in range(STEP_TILES):
-                nc.vector.bn_stats(out=stats[:, t, :], in_=step_tiles[s]["sums"][t][:])
-            for t in range(STEP_TILES):
-                nc.vector.bn_aggr(out=mean_var[:, t, :], in_=stats[:, t, :])
-            step_tiles[s]["mean_var"] = mean_var
-
-        def standard_deviation(s):
-            std = small.tile([P, STEP_TILES], F32)
-            nc.scalar.sqrt(out=std[:], in_=step_tiles[s]["mean_var"][:, :, 1])
-            step_tiles[s]["std"] = std
-
-        def add_eps(s):
-            minus_std = small.tile([P, STEP_TILES], F32)
-            nc.vector.tensor_scalar(
-                out=minus_std[:], in0=step_tiles[s]["std"][:], scalar1=-1.0, scalar2=EPS,
-                op0=ALU.mult, op1=ALU.subtract,
+        def add_mu_to_internal(i):
+            drive = tiles[i + 3]["grouped"][:, 0 : 2 * H].bitcast(F32)
+            nc.gpsimd.tensor_tensor(
+                out=drive,
+                in0=groups[i // GROUP_TILES]["internal"][:, i % GROUP_TILES, :],
+                in1=mu_all[:],
+                op=ALU.add,
             )
-            step_tiles[s]["minus_std"] = minus_std
+            tiles[i]["drive"] = drive
 
-        def scale_and_add(s):
-            minus_inv = small.tile([P, STEP_TILES], F32)
-            minus_hy = results.tile([P, STEP_TILES, H], F32)
-            nc.vector.reciprocal(out=minus_inv[:], in_=step_tiles[s]["minus_std"][:])
-            for t in range(STEP_TILES):
-                nc.vector.scalar_tensor_tensor(
-                    out=minus_hy[:, t, :],
-                    in0=step_tiles[s]["sums"][t][:],
-                    scalar=minus_inv[:, t : t + 1],
-                    in1=step_tiles[s]["drive"][t][:],
-                    op0=ALU.mult,
-                    op1=ALU.subtract,
-                )
-            step_tiles[s]["minus_inv"] = minus_inv
-            step_tiles[s]["hy"] = minus_hy
+        def statistics(i):
+            stats = small.tile([P, 6], F32)
+            nc.vector.bn_stats(out=stats[:], in_=tiles[i]["sums"][:])
+            tiles[i]["stats"] = stats
 
-        def shift_by_mean(s):
-            shift = small.tile([P, STEP_TILES], F32)
-            for t in range(STEP_TILES):
-                nc.scalar.activation(
-                    out=shift[:, t : t + 1],
-                    in_=step_tiles[s]["mean_var"][:, t, 0:1],
-                    func=ACT.Copy,
-                    scale=step_tiles[s]["minus_inv"][:, t : t + 1],
-                )
-            step_tiles[s]["shift"] = shift
+        def mean_and_variance(i):
+            mean_var = small.tile([P, 2], F32)
+            nc.vector.bn_aggr(out=mean_var[:], in_=tiles[i]["stats"][:])
+            tiles[i]["mean_var"] = mean_var
 
-        def relu(s, t):
-            hy, shift = step_tiles[s]["hy"], step_tiles[s]["shift"]
+        def standard_deviation(i):
+            std = small.tile([P, 1], F32)
+            nc.scalar.sqrt(out=std[:], in_=tiles[i]["mean_var"][:, 1:2])
+            tiles[i]["std"] = std
+
+        def add_eps(i):
+            minus_std = small.tile([P, 1], F32)
             nc.scalar.activation(
-                out=hy[:, t, :], in_=hy[:, t, :], func=ACT.Relu, bias=shift[:, t : t + 1], scale=-1.0
+                out=minus_std[:], in_=tiles[i]["std"][:], func=ACT.Copy, scale=-1.0, bias=-EPS
+            )
+            tiles[i]["minus_std"] = minus_std
+
+        def invert(i):
+            minus_inv = small.tile([P, 1], F32)
+            nc.vector.reciprocal(out=minus_inv[:], in_=tiles[i]["minus_std"][:])
+            tiles[i]["minus_inv"] = minus_inv
+
+        def scale_and_add(i):
+            if i % STORE_TILES == 0:
+                minus_hy = results.tile([P, STORE_TILES, H], F32)
+            else:
+                minus_hy = tiles[i - 1]["minus_hy"]
+            nc.vector.scalar_tensor_tensor(
+                out=minus_hy[:, i % STORE_TILES, :],
+                in0=tiles[i]["sums"][:],
+                scalar=tiles[i]["minus_inv"][:],
+                in1=tiles[i]["drive"],
+                op0=ALU.mult,
+                op1=ALU.subtract,
+            )
+            tiles[i]["minus_hy"] = minus_hy
+
+        def shift_by_mean(i):
+            shift = small.tile([P, 1], F32)
+            nc.scalar.activation(
+                out=shift[:], in_=tiles[i]["mean_var"][:, 0:1], func=ACT.Copy,
+                scale=tiles[i]["minus_inv"][:],
+            )
+            tiles[i]["shift"] = shift
+
+        def relu(i):
+            hy = tiles[i]["minus_hy"][:, i % STORE_TILES, :]
+            nc.scalar.activation(
+                out=hy, in_=hy, func=ACT.Relu, bias=tiles[i]["shift"][:], scale=-1.0
             )
 
-        def store(s):
-            nc.scalar.dma_start(
-                out=out_steps[s], in_=step_tiles[s]["hy"][:].rearrange("p t h -> p (t h)")
+        def store(i):
+            last = i % GROUP_TILES + 1
+            nc.sync.dma_start(
+                out=out_groups[i // GROUP_TILES][:, last - STORE_TILES : last, :],
+                in_=tiles[i]["minus_hy"][:],
             )
 
-        for s in range(2):
-            for t in range(STEP_TILES):
-                turn(s, t)
-        for t in range(STEP_TILES):
-            quantise(0, t)
-            multiply(0, t)
-        for t in range(STEP_TILES):
-            turn(2, t)
-            quantise(1, t)
-        for k in range(STEPS + 1):
-            if k + STEPS_AHEAD < STEPS:
-                load_step(k + STEPS_AHEAD)
-            if k < STEPS:
-                add_mu_to_internal(k)
-                mean_and_variance(k)
-            if k >= 1:
-                shift_by_mean(k - 1)
-            for t in range(STEP_TILES):
-                if k + 3 < STEPS:
-                    turn(k + 3, t)
-                if t == 0 and k < STEPS:
-                    standard_deviation(k)
-                if k + 1 < STEPS:
-                    multiply(k + 1, t)
-                if k >= 1:
-                    relu(k - 1, t)
-            if k >= 1:
-                store(k - 1)
-            if k < STEPS:
-                if k + 2 < STEPS:
-                    quantise(k + 2, 0)
+        def exists(i):
+            return 0 <= i < TILES
+
+        for k in range(-5, TILES + 3):
+            g = GROUP_BUFS + (k + 1) // GROUP_TILES
+            if (k + 1) % GROUP_TILES == 0 and GROUP_BUFS <= g < GROUPS:
+                load_activations(g, 1)
+            g = GROUP_BUFS - 1 + k // GROUP_TILES
+            if k % GROUP_TILES == 0 and GROUP_BUFS <= g < GROUPS:
+                load_internal(g)
+
+            if k < 0 and exists(k + 2):
+                multiply(k + 2)
+            if exists(k - 2):
+                shift_by_mean(k - 2)
+            if exists(k):
+                standard_deviation(k)
+            if k + 5 < TILES + 3:
+                new_grouped(k + 5)
+            if exists(k + 5):
+                turn(k + 5, 0)
+            if exists(k):
                 add_eps(k)
-                if k + 2 < STEPS:
-                    quantise(k + 2, 1)
-                scale_and_add(k)
+            if exists(k - 2):
+                relu(k - 2)
+                if (k - 1) % STORE_TILES == 0:
+                    store(k - 2)
+            if exists(k + 5):
+                turn(k + 5, 1)
+            if k >= 0 and exists(k + 2):
+                multiply(k + 2)
+            if exists(k + 3):
+                quantise(k + 3)
+            if exists(k):
+                add_mu_to_internal(k)
+            if exists(k + 1):
+                statistics(k + 1)
+            if exists(k):
+                invert(k)
+            if exists(k - 1):
+                scale_and_add(k - 1)
+            if exists(k + 1):
+                mean_and_variance(k + 1)

@@ -35,7 +35,7 @@ def as_words(tile_2d, row_tiles):
     return tile_2d[:].bitcast(F32).rearrange("p (t w) -> p t w", t=row_tiles)
 
 
-def turn_into_bank(nc, turn_banks, identity, two_sources, grouped_words, copy_out):
+def turn_into_bank(nc, turn_banks, identity, two_sources):
     turned = turn_banks.tile([P, 2, 2, P], F32)
     for i in range(2):
         for u in range(2):
@@ -44,6 +44,10 @@ def turn_into_bank(nc, turn_banks, identity, two_sources, grouped_words, copy_ou
                 in_=two_sources[i][:, u * P : (u + 1) * P],
                 identity=identity[:],
             )
+    return turned
+
+
+def empty_bank(turned, grouped_words, copy_out):
     copy_out(out=grouped_words, in_=turned[:].rearrange("p g u r -> p g r u"))
 
 
@@ -65,13 +69,13 @@ def tile_sparsegatedrnncell_pb_t_kernel(
         loads = stack.enter_context(tc.tile_pool(name="loads", bufs=GROUP_BUFS))
         regroup = stack.enter_context(tc.tile_pool(name="regroup", bufs=5))
         packed = stack.enter_context(tc.tile_pool(name="packed", bufs=4))
-        results = stack.enter_context(tc.tile_pool(name="results", bufs=4))
+        results = stack.enter_context(tc.tile_pool(name="results", bufs=8))
         small = stack.enter_context(tc.tile_pool(name="small", bufs=6))
         turn_banks = stack.enter_context(tc.psum_pool(name="turn_banks", bufs=4))
         sum_banks = stack.enter_context(tc.psum_pool(name="sum_banks", bufs=4))
 
         groups = {}
-        tiles = {}
+        tiles = {i: {} for i in range(TILES + 3)}
 
         def load_activations(g, parts):
             x_sb = loads.tile([P, GROUP_TILES * K_PASS], BF16)
@@ -140,13 +144,13 @@ def tile_sparsegatedrnncell_pb_t_kernel(
         )
         for g in range(PASSES):
             for j in range(0, H_TILES, 2):
-                turn_into_bank(
-                    nc,
-                    turn_banks,
-                    identity,
-                    [w_words[g][:, j, :], w_words[g][:, j + 1, :]],
+                turned = turn_into_bank(
+                    nc, turn_banks, identity, [w_words[g][:, j, :], w_words[g][:, j + 1, :]]
+                )
+                empty_bank(
+                    turned,
                     w_grouped_words[:, g, j : j + 2, :, :],
-                    nc.scalar.copy if j == 0 else nc.vector.tensor_copy,
+                    nc.vector.tensor_copy if j > 0 and g < 2 else nc.scalar.copy,
                 )
             one_pass = slice(g * H, (g + 1) * H)
             nc.vector.quantize_mx(
@@ -155,29 +159,36 @@ def tile_sparsegatedrnncell_pb_t_kernel(
                 in_=w_grouped[:, g * H * PACK : (g + 1) * H * PACK],
             )
 
-        mu_bank = sum_banks.tile([P, H], F32, tag="sums")
-        nc.tensor.matmul(out=mu_bank[:], lhsT=ones[:], rhs=mu_row[:], start=True, stop=True)
         mu_all = consts.tile([P, H], F32)
-        nc.scalar.copy(out=mu_all[:], in_=mu_bank[:])
+
+        def spread_mu():
+            mu_bank = turn_banks.tile([P, H], F32, tag="turned")
+            nc.tensor.matmul(out=mu_bank[:], lhsT=ones[:], rhs=mu_row[:], start=True, stop=True)
+            nc.scalar.copy(out=mu_all[:], in_=mu_bank[:])
 
         def new_grouped(i):
             grouped = regroup.tile([P, TILE_WORDS * PACK], BF16, align_bytes=64)
-            tiles[i] = {"grouped": grouped}
+            tiles[i]["grouped"] = grouped
 
-        def turn(i, pair):
+        def turn(i):
             group, t = groups[i // GROUP_TILES], i % GROUP_TILES
-            if pair == 0:
-                two_passes = [group["x"][:, t, :], group["hx"][:, t, :]]
-            else:
-                two_passes = [group["sy"][:, t, 0:WORDS], group["sy"][:, t, WORDS : 2 * WORDS]]
+            four_passes = [
+                group["x"][:, t, :],
+                group["hx"][:, t, :],
+                group["sy"][:, t, 0:WORDS],
+                group["sy"][:, t, WORDS : 2 * WORDS],
+            ]
+            tiles[i]["turned"] = [
+                turn_into_bank(nc, turn_banks, identity, four_passes[2 * pair : 2 * pair + 2])
+                for pair in range(PASSES // 2)
+            ]
+
+        def regroup_pair(i, pair):
             grouped_words = tiles[i]["grouped"][:].bitcast(F32).rearrange(
                 "p (g r u) -> p g r u", g=PASSES, r=P, u=2
             )
-            turn_into_bank(
-                nc,
-                turn_banks,
-                identity,
-                two_passes,
+            empty_bank(
+                tiles[i]["turned"][pair],
                 grouped_words[:, 2 * pair : 2 * pair + 2, :, :],
                 nc.scalar.copy,
             )
@@ -283,16 +294,32 @@ def tile_sparsegatedrnncell_pb_t_kernel(
         def exists(i):
             return 0 <= i < TILES
 
-        for k in range(-5, TILES + 3):
-            g = GROUP_BUFS + (k + 1) // GROUP_TILES
-            if (k + 1) % GROUP_TILES == 0 and GROUP_BUFS <= g < GROUPS:
+        for i in range(5):
+            if i >= 2:
+                quantise(i - 2)
+            if 2 <= i < 4:
+                multiply(i - 2)
+            turn(i)
+            new_grouped(i)
+            regroup_pair(i, 0)
+            regroup_pair(i, 1)
+            if i == 3:
+                spread_mu()
+        statistics(0)
+        mean_and_variance(0)
+
+        for k in range(TILES + 3):
+            g = GROUP_BUFS + k // GROUP_TILES
+            if k % GROUP_TILES == 0 and g < GROUPS:
                 load_activations(g, 1)
             g = GROUP_BUFS - 1 + k // GROUP_TILES
             if k % GROUP_TILES == 0 and GROUP_BUFS <= g < GROUPS:
                 load_internal(g)
 
-            if k < 0 and exists(k + 2):
-                multiply(k + 2)
+            if k % 2 == 0:
+                for i in (k + 5, k + 6):
+                    if exists(i):
+                        turn(i)
             if exists(k - 2):
                 shift_by_mean(k - 2)
             if exists(k):
@@ -300,7 +327,7 @@ def tile_sparsegatedrnncell_pb_t_kernel(
             if k + 5 < TILES + 3:
                 new_grouped(k + 5)
             if exists(k + 5):
-                turn(k + 5, 0)
+                regroup_pair(k + 5, 0)
             if exists(k):
                 add_eps(k)
             if exists(k - 2):
@@ -308,9 +335,7 @@ def tile_sparsegatedrnncell_pb_t_kernel(
                 if (k - 1) % STORE_TILES == 0:
                     store(k - 2)
             if exists(k + 5):
-                turn(k + 5, 1)
-            if k >= 0 and exists(k + 2):
-                multiply(k + 2)
+                regroup_pair(k + 5, 1)
             if exists(k + 3):
                 quantise(k + 3)
             if exists(k):
@@ -321,5 +346,9 @@ def tile_sparsegatedrnncell_pb_t_kernel(
                 invert(k)
             if exists(k - 1):
                 scale_and_add(k - 1)
+            if k % 2 == 0:
+                for i in (k + 2, k + 3):
+                    if exists(i):
+                        multiply(i)
             if exists(k + 1):
                 mean_and_variance(k + 1)

@@ -26,6 +26,7 @@ TILES = ROWS // P
 GROUP_TILES = 4
 GROUPS = TILES // GROUP_TILES
 GROUP_BUFS = 4
+DRIVES_AHEAD = 8
 STORE_TILES = 2
 
 FLOPS = 2 * ROWS * PASSES * K_PASS * H
@@ -70,12 +71,13 @@ def tile_sparsegatedrnncell_pb_t_kernel(
         regroup = stack.enter_context(tc.tile_pool(name="regroup", bufs=5))
         packed = stack.enter_context(tc.tile_pool(name="packed", bufs=4))
         results = stack.enter_context(tc.tile_pool(name="results", bufs=8))
+        drives = stack.enter_context(tc.tile_pool(name="drives", bufs=DRIVES_AHEAD + 3))
         small = stack.enter_context(tc.tile_pool(name="small", bufs=6))
         turn_banks = stack.enter_context(tc.psum_pool(name="turn_banks", bufs=4))
         sum_banks = stack.enter_context(tc.psum_pool(name="sum_banks", bufs=4))
 
         groups = {}
-        tiles = {i: {} for i in range(TILES + 3)}
+        tiles = {i: {} for i in range(TILES)}
 
         def load_activations(g, parts):
             x_sb = loads.tile([P, GROUP_TILES * K_PASS], BF16)
@@ -219,9 +221,9 @@ def tile_sparsegatedrnncell_pb_t_kernel(
             tiles[i]["sums"] = sums
 
         def add_mu_to_internal(i):
-            drive = tiles[i + 3]["grouped"][:, 0 : 2 * H].bitcast(F32)
+            drive = drives.tile([P, H], F32)
             nc.gpsimd.tensor_tensor(
-                out=drive,
+                out=drive[:],
                 in0=groups[i // GROUP_TILES]["internal"][:, i % GROUP_TILES, :],
                 in1=mu_all[:],
                 op=ALU.add,
@@ -264,7 +266,7 @@ def tile_sparsegatedrnncell_pb_t_kernel(
                 out=minus_hy[:, i % STORE_TILES, :],
                 in0=tiles[i]["sums"][:],
                 scalar=tiles[i]["minus_inv"][:],
-                in1=tiles[i]["drive"],
+                in1=tiles[i]["drive"][:],
                 op0=ALU.mult,
                 op1=ALU.subtract,
             )
@@ -307,13 +309,13 @@ def tile_sparsegatedrnncell_pb_t_kernel(
                 spread_mu()
         statistics(0)
         mean_and_variance(0)
+        for i in range(DRIVES_AHEAD):
+            add_mu_to_internal(i)
 
         for k in range(TILES + 3):
             g = GROUP_BUFS + k // GROUP_TILES
             if k % GROUP_TILES == 0 and g < GROUPS:
                 load_activations(g, 1)
-            g = GROUP_BUFS - 1 + k // GROUP_TILES
-            if k % GROUP_TILES == 0 and GROUP_BUFS <= g < GROUPS:
                 load_internal(g)
 
             if k % 2 == 0:
@@ -324,9 +326,8 @@ def tile_sparsegatedrnncell_pb_t_kernel(
                 shift_by_mean(k - 2)
             if exists(k):
                 standard_deviation(k)
-            if k + 5 < TILES + 3:
-                new_grouped(k + 5)
             if exists(k + 5):
+                new_grouped(k + 5)
                 regroup_pair(k + 5, 0)
             if exists(k):
                 add_eps(k)
@@ -338,8 +339,8 @@ def tile_sparsegatedrnncell_pb_t_kernel(
                 regroup_pair(k + 5, 1)
             if exists(k + 3):
                 quantise(k + 3)
-            if exists(k):
-                add_mu_to_internal(k)
+            if exists(k + DRIVES_AHEAD):
+                add_mu_to_internal(k + DRIVES_AHEAD)
             if exists(k + 1):
                 statistics(k + 1)
             if exists(k):

@@ -79,14 +79,16 @@ def tile_sparsegatedrnncell_pb_t_kernel(
         groups = {}
         tiles = {i: {} for i in range(TILES)}
 
-        def load_activations(g, parts):
+        def load_group(g, parts):
             x_sb = loads.tile([P, GROUP_TILES * K_PASS], BF16)
             hx_sb = loads.tile([P, GROUP_TILES * K_PASS], BF16)
             sy_sb = loads.tile([P, GROUP_TILES * 2 * K_PASS], BF16)
+            internal_sb = loads.tile([P, GROUP_TILES, H], BF16)
             groups[g] = {
                 "x": as_words(x_sb, GROUP_TILES),
                 "hx": as_words(hx_sb, GROUP_TILES),
                 "sy": as_words(sy_sb, GROUP_TILES),
+                "internal": internal_sb,
             }
             wide = GROUP_TILES // parts
             for part in range(parts):
@@ -96,11 +98,8 @@ def tile_sparsegatedrnncell_pb_t_kernel(
                         out=sb[:].rearrange("p (t k) -> p t k", t=GROUP_TILES)[:, t, :],
                         in_=dram[g][:, t, :],
                     )
-
-        def load_internal(g):
-            internal_sb = loads.tile([P, GROUP_TILES, H], BF16)
-            nc.sync.dma_start(out=internal_sb[:], in_=internal_groups[g])
-            groups[g]["internal"] = internal_sb
+                if part == 0:
+                    nc.sync.dma_start(out=internal_sb[:], in_=internal_groups[g])
 
         mu_row = consts.tile([P, H], BF16)
         nc.vector.memset(mu_row[:], 0.0)
@@ -117,10 +116,7 @@ def tile_sparsegatedrnncell_pb_t_kernel(
                 in_=w_dram.rearrange("(j p) k -> p j k", p=P),
             )
         for g in range(GROUP_BUFS):
-            load_activations(g, 2 if g < 2 else 1)
-            if g >= 1:
-                load_internal(g - 1)
-        load_internal(GROUP_BUFS - 1)
+            load_group(g, 2 if g < 2 else 1)
 
         identity = consts.tile([P, P], F32)
         make_identity(nc, identity[:])
@@ -286,11 +282,11 @@ def tile_sparsegatedrnncell_pb_t_kernel(
                 out=hy, in_=hy, func=ACT.Relu, bias=tiles[i]["shift"][:], scale=-1.0
             )
 
-        def store(i):
-            last = i % GROUP_TILES + 1
+        def store(i, width):
+            last, last_in_group = i % STORE_TILES + 1, i % GROUP_TILES + 1
             nc.sync.dma_start(
-                out=out_groups[i // GROUP_TILES][:, last - STORE_TILES : last, :],
-                in_=tiles[i]["minus_hy"][:],
+                out=out_groups[i // GROUP_TILES][:, last_in_group - width : last_in_group, :],
+                in_=tiles[i]["minus_hy"][:, last - width : last, :],
             )
 
         def exists(i):
@@ -305,7 +301,7 @@ def tile_sparsegatedrnncell_pb_t_kernel(
             new_grouped(i)
             regroup_pair(i, 0)
             regroup_pair(i, 1)
-            if i == 3:
+            if i == 1:
                 spread_mu()
         statistics(0)
         mean_and_variance(0)
@@ -315,8 +311,7 @@ def tile_sparsegatedrnncell_pb_t_kernel(
         for k in range(TILES + 3):
             g = GROUP_BUFS + k // GROUP_TILES
             if k % GROUP_TILES == 0 and g < GROUPS:
-                load_activations(g, 1)
-                load_internal(g)
+                load_group(g, 1)
 
             if k % 2 == 0:
                 for i in (k + 5, k + 6):
@@ -333,8 +328,10 @@ def tile_sparsegatedrnncell_pb_t_kernel(
                 add_eps(k)
             if exists(k - 2):
                 relu(k - 2)
-                if (k - 1) % STORE_TILES == 0:
-                    store(k - 2)
+                if k - 2 >= TILES - STORE_TILES:
+                    store(k - 2, 1)
+                elif (k - 1) % STORE_TILES == 0:
+                    store(k - 2, STORE_TILES)
             if exists(k + 5):
                 regroup_pair(k + 5, 1)
             if exists(k + 3):
@@ -343,10 +340,10 @@ def tile_sparsegatedrnncell_pb_t_kernel(
                 add_mu_to_internal(k + DRIVES_AHEAD)
             if exists(k + 1):
                 statistics(k + 1)
-            if exists(k):
-                invert(k)
             if exists(k - 1):
                 scale_and_add(k - 1)
+            if exists(k):
+                invert(k)
             if k % 2 == 0:
                 for i in (k + 2, k + 3):
                     if exists(i):

@@ -313,10 +313,8 @@ def tile_sparsegatedrnncell_pb_t_kernel(
             if k % GROUP_TILES == 0 and g < GROUPS:
                 load_group(g, 1)
 
-            if k % 2 == 0:
-                for i in (k + 5, k + 6):
-                    if exists(i):
-                        turn(i)
+            if exists(k + 5):
+                turn(k + 5)
             if exists(k - 2):
                 shift_by_mean(k - 2)
             if exists(k):
@@ -344,9 +342,7 @@ def tile_sparsegatedrnncell_pb_t_kernel(
                 scale_and_add(k - 1)
             if exists(k):
                 invert(k)
-            if k % 2 == 0:
-                for i in (k + 2, k + 3):
-                    if exists(i):
-                        multiply(i)
+            if exists(k + 2):
+                multiply(k + 2)
             if exists(k + 1):
                 mean_and_variance(k + 1)

@@ -26,7 +26,6 @@ TILES = ROWS // P
 GROUP_TILES = 4
 GROUPS = TILES // GROUP_TILES
 GROUP_BUFS = 4
-DRIVES_AHEAD = 8
 STORE_TILES = 2
 
 FLOPS = 2 * ROWS * PASSES * K_PASS * H
@@ -71,7 +70,7 @@ def tile_sparsegatedrnncell_pb_t_kernel(
         regroup = stack.enter_context(tc.tile_pool(name="regroup", bufs=5))
         packed = stack.enter_context(tc.tile_pool(name="packed", bufs=4))
         results = stack.enter_context(tc.tile_pool(name="results", bufs=8))
-        drives = stack.enter_context(tc.tile_pool(name="drives", bufs=DRIVES_AHEAD + 3))
+        drives = stack.enter_context(tc.tile_pool(name="drives", bufs=GROUP_TILES))
         small = stack.enter_context(tc.tile_pool(name="small", bufs=6))
         turn_banks = stack.enter_context(tc.psum_pool(name="turn_banks", bufs=4))
         sum_banks = stack.enter_context(tc.psum_pool(name="sum_banks", bufs=4))
@@ -79,7 +78,7 @@ def tile_sparsegatedrnncell_pb_t_kernel(
         groups = {}
         tiles = {i: {} for i in range(TILES)}
 
-        def load_group(g, parts):
+        def load_group(g, widths):
             x_sb = loads.tile([P, GROUP_TILES * K_PASS], BF16)
             hx_sb = loads.tile([P, GROUP_TILES * K_PASS], BF16)
             sy_sb = loads.tile([P, GROUP_TILES * 2 * K_PASS], BF16)
@@ -90,16 +89,16 @@ def tile_sparsegatedrnncell_pb_t_kernel(
                 "sy": as_words(sy_sb, GROUP_TILES),
                 "internal": internal_sb,
             }
-            wide = GROUP_TILES // parts
-            for part in range(parts):
-                t = slice(part * wide, (part + 1) * wide)
+            first = 0
+            for width in widths:
+                t = slice(first, first + width)
+                first += width
                 for sb, dram in ((x_sb, x_groups), (hx_sb, hx_groups), (sy_sb, sy_groups)):
                     nc.sync.dma_start(
                         out=sb[:].rearrange("p (t k) -> p t k", t=GROUP_TILES)[:, t, :],
                         in_=dram[g][:, t, :],
                     )
-                if part == 0:
-                    nc.sync.dma_start(out=internal_sb[:], in_=internal_groups[g])
+            nc.sync.dma_start(out=internal_sb[:], in_=internal_groups[g])
 
         mu_row = consts.tile([P, H], BF16)
         nc.vector.memset(mu_row[:], 0.0)
@@ -110,13 +109,17 @@ def tile_sparsegatedrnncell_pb_t_kernel(
         w_ih_sb = consts.tile([P, H_TILES * K_PASS], BF16)
         w_hh_sb = consts.tile([P, H_TILES * K_PASS], BF16)
         w_sh_sb = consts.tile([P, H_TILES * 2 * K_PASS], BF16)
-        for w_sb, w_dram in ((w_ih_sb, W_ih), (w_hh_sb, W_hh), (w_sh_sb, W_sh)):
-            nc.sync.dma_start(
-                out=w_sb[:].rearrange("p (j k) -> p j k", j=H_TILES),
-                in_=w_dram.rearrange("(j p) k -> p j k", p=P),
-            )
-        for g in range(GROUP_BUFS):
-            load_group(g, 2 if g < 2 else 1)
+        for w_sb, w_dram, parts in ((w_ih_sb, W_ih, 1), (w_hh_sb, W_hh, 1), (w_sh_sb, W_sh, 2)):
+            wide = H_TILES // parts
+            for j in range(0, H_TILES, wide):
+                nc.sync.dma_start(
+                    out=w_sb[:].rearrange("p (j k) -> p j k", j=H_TILES)[:, j : j + wide, :],
+                    in_=w_dram.rearrange("(p j) k -> p j k", j=H_TILES)[:, j : j + wide, :],
+                )
+        load_group(0, (1, 1, 2))
+        for g in range(1, GROUP_BUFS - 1):
+            load_group(g, (2, 2))
+        load_group(GROUP_BUFS - 1, (GROUP_TILES,))
 
         identity = consts.tile([P, P], F32)
         make_identity(nc, identity[:])
@@ -129,7 +132,7 @@ def tile_sparsegatedrnncell_pb_t_kernel(
         w_codes = consts.tile([P, PASSES * H], U32, align_bytes=64)
         w_scales = consts.tile([P, PASSES * H], U8, align_bytes=64)
         w_grouped_words = w_grouped[:].bitcast(F32).rearrange(
-            "p (g j r u) -> p g j r u", g=PASSES, j=H_TILES, r=P, u=2
+            "p (g r j u) -> p g r j u", g=PASSES, r=P, j=H_TILES, u=2
         )
         w_ih_words = as_words(w_ih_sb, H_TILES)
         w_hh_words = as_words(w_hh_sb, H_TILES)
@@ -140,29 +143,29 @@ def tile_sparsegatedrnncell_pb_t_kernel(
             w_sh_words[:, :, 0:WORDS],
             w_sh_words[:, :, WORDS : 2 * WORDS],
         )
-        for g in range(PASSES):
-            for j in range(0, H_TILES, 2):
-                turned = turn_into_bank(
-                    nc, turn_banks, identity, [w_words[g][:, j, :], w_words[g][:, j + 1, :]]
-                )
-                empty_bank(
-                    turned,
-                    w_grouped_words[:, g, j : j + 2, :, :],
-                    nc.vector.tensor_copy if j > 0 and g < 2 else nc.scalar.copy,
-                )
-            one_pass = slice(g * H, (g + 1) * H)
-            nc.vector.quantize_mx(
-                out=w_codes[:, one_pass].bitcast(FP8X4),
-                scales=w_scales[:, one_pass],
-                in_=w_grouped[:, g * H * PACK : (g + 1) * H * PACK],
+        for g, j in ((0, 0), (0, 2), (1, 0), (1, 2), (2, 0), (3, 0), (2, 2), (3, 2)):
+            turned = turn_into_bank(
+                nc, turn_banks, identity, [w_words[g][:, j, :], w_words[g][:, j + 1, :]]
             )
+            copy_out = nc.vector.tensor_copy if (g, j) in ((0, 2), (1, 2), (3, 0)) else nc.scalar.copy
+            copy_out(
+                out=w_grouped_words[:, g, :, j : j + 2, :],
+                in_=turned[:].rearrange("p j u r -> p r j u"),
+            )
+            if j == 2:
+                one_pass = slice(g * H, (g + 1) * H)
+                nc.vector.quantize_mx(
+                    out=w_codes[:, one_pass].bitcast(FP8X4),
+                    scales=w_scales[:, one_pass],
+                    in_=w_grouped[:, g * H * PACK : (g + 1) * H * PACK],
+                )
 
         mu_all = consts.tile([P, H], F32)
 
         def spread_mu():
-            mu_bank = turn_banks.tile([P, H], F32, tag="turned")
+            mu_bank = sum_banks.tile([P, H], F32, tag="sums")
             nc.tensor.matmul(out=mu_bank[:], lhsT=ones[:], rhs=mu_row[:], start=True, stop=True)
-            nc.scalar.copy(out=mu_all[:], in_=mu_bank[:])
+            return mu_bank
 
         def new_grouped(i):
             grouped = regroup.tile([P, TILE_WORDS * PACK], BF16, align_bytes=64)
@@ -216,12 +219,12 @@ def tile_sparsegatedrnncell_pb_t_kernel(
                 )
             tiles[i]["sums"] = sums
 
-        def add_mu_to_internal(i):
+        def add_mu_to_internal(i, add, mu_source):
             drive = drives.tile([P, H], F32)
-            nc.gpsimd.tensor_tensor(
+            add(
                 out=drive[:],
                 in0=groups[i // GROUP_TILES]["internal"][:, i % GROUP_TILES, :],
-                in1=mu_all[:],
+                in1=mu_source[:],
                 op=ALU.add,
             )
             tiles[i]["drive"] = drive
@@ -292,57 +295,83 @@ def tile_sparsegatedrnncell_pb_t_kernel(
         def exists(i):
             return 0 <= i < TILES
 
-        for i in range(5):
-            if i >= 2:
-                quantise(i - 2)
-            if 2 <= i < 4:
-                multiply(i - 2)
+        turn(0)
+        new_grouped(0)
+        regroup_pair(0, 0)
+        regroup_pair(0, 1)
+        turn(1)
+        new_grouped(1)
+        regroup_pair(1, 0)
+        regroup_pair(1, 1)
+        mu_bank = spread_mu()
+        quantise(0)
+        multiply(0)
+        quantise(1)
+        for i in (2, 3):
             turn(i)
             new_grouped(i)
             regroup_pair(i, 0)
             regroup_pair(i, 1)
-            if i == 1:
-                spread_mu()
+        multiply(1)
         statistics(0)
         mean_and_variance(0)
-        for i in range(DRIVES_AHEAD):
-            add_mu_to_internal(i)
+        add_mu_to_internal(0, nc.vector.tensor_tensor, mu_bank)
+        quantise(2)
+        for i in range(1, GROUP_TILES):
+            add_mu_to_internal(i, nc.vector.tensor_tensor, mu_bank)
+        standard_deviation(0)
+        add_eps(0)
+        nc.scalar.copy(out=mu_all[:], in_=mu_bank[:])
+        turn(4)
+        new_grouped(4)
+        regroup_pair(4, 0)
+        regroup_pair(4, 1)
 
         for k in range(TILES + 3):
-            g = GROUP_BUFS + k // GROUP_TILES
-            if k % GROUP_TILES == 0 and g < GROUPS:
-                load_group(g, 1)
-
             if exists(k + 5):
                 turn(k + 5)
+
+            if k == 1:
+                invert(0)
+                scale_and_add(0)
+            if exists(k + 3):
+                quantise(k + 3)
+            if 1 <= k < TILES - 1:
+                mean_and_variance(k)
+            if k > 1 and exists(k - 1):
+                invert(k - 1)
+
             if exists(k - 2):
                 shift_by_mean(k - 2)
-            if exists(k):
-                standard_deviation(k)
             if exists(k + 5):
                 new_grouped(k + 5)
                 regroup_pair(k + 5, 0)
-            if exists(k):
-                add_eps(k)
+            if k >= 1 and exists(k):
+                standard_deviation(k)
             if exists(k - 2):
                 relu(k - 2)
                 if k - 2 >= TILES - STORE_TILES:
                     store(k - 2, 1)
                 elif (k - 1) % STORE_TILES == 0:
                     store(k - 2, STORE_TILES)
+            if k >= 1 and exists(k):
+                add_eps(k)
             if exists(k + 5):
                 regroup_pair(k + 5, 1)
-            if exists(k + 3):
-                quantise(k + 3)
-            if exists(k + DRIVES_AHEAD):
-                add_mu_to_internal(k + DRIVES_AHEAD)
+
             if exists(k + 1):
                 statistics(k + 1)
-            if exists(k - 1):
+            if k + 1 == TILES - 1:
+                mean_and_variance(k + 1)
+            if k > 1 and exists(k - 1):
                 scale_and_add(k - 1)
-            if exists(k):
-                invert(k)
+
+            if exists(k + 3) and k + 3 >= GROUP_TILES:
+                add_mu_to_internal(k + 3, nc.gpsimd.tensor_tensor, mu_all)
+
             if exists(k + 2):
                 multiply(k + 2)
-            if exists(k + 1):
-                mean_and_variance(k + 1)
+
+            g = GROUP_BUFS + k // GROUP_TILES
+            if k % GROUP_TILES == 0 and g < GROUPS:
+                load_group(g, (GROUP_TILES,))

@@ -143,10 +143,22 @@ def tile_sparsegatedrnncell_pb_t_kernel(
             w_sh_words[:, :, 0:WORDS],
             w_sh_words[:, :, WORDS : 2 * WORDS],
         )
+        filler = consts.tile([P, H], BF16)
+        nc.vector.memset(filler[:], 0.0)
+        filler_bank = sum_banks.tile([P, H], F32, tag="sums")
+
+        def keep_tensor_clock_up(matmuls):
+            for i in range(matmuls):
+                nc.tensor.matmul(
+                    out=filler_bank[:], lhsT=filler[:, 0:P], rhs=filler[:], start=True, stop=True
+                )
+
+        keep_tensor_clock_up(5)
         for g, j in ((0, 0), (0, 2), (1, 0), (1, 2), (2, 0), (3, 0), (2, 2), (3, 2)):
             turned = turn_into_bank(
                 nc, turn_banks, identity, [w_words[g][:, j, :], w_words[g][:, j + 1, :]]
             )
+            keep_tensor_clock_up(1)
             copy_out = nc.vector.tensor_copy if (g, j) in ((0, 2), (1, 2), (3, 0)) else nc.scalar.copy
             copy_out(
                 out=w_grouped_words[:, g, :, j : j + 2, :],
@@ -304,8 +316,10 @@ def tile_sparsegatedrnncell_pb_t_kernel(
         regroup_pair(1, 0)
         regroup_pair(1, 1)
         mu_bank = spread_mu()
+        keep_tensor_clock_up(1)
         quantise(0)
         multiply(0)
+        keep_tensor_clock_up(0)
         quantise(1)
         for i in (2, 3):
             turn(i)
@@ -348,13 +362,15 @@ def tile_sparsegatedrnncell_pb_t_kernel(
                 regroup_pair(k + 5, 0)
             if k >= 1 and exists(k):
                 standard_deviation(k)
+            if k == TILES - 1:
+                add_eps(k)
             if exists(k - 2):
                 relu(k - 2)
-                if k - 2 >= TILES - STORE_TILES:
+                if k - 2 >= TILES - 4:
                     store(k - 2, 1)
                 elif (k - 1) % STORE_TILES == 0:
                     store(k - 2, STORE_TILES)
-            if k >= 1 and exists(k):
+            if 1 <= k < TILES - 1:
                 add_eps(k)
             if exists(k + 5):
                 regroup_pair(k + 5, 1)

from contextlib import ExitStack

import concourse.mybir as mybir
from concourse.masks import make_identity

F32 = mybir.dt.float32
BF16 = mybir.dt.bfloat16
U32 = mybir.dt.uint32
U8 = mybir.dt.uint8
FP8X4 = mybir.dt.float8_e4m3fn_x4
ALU = mybir.AluOpType
ACT = mybir.ActivationFunctionType

P = 128
PACK = 4
K_PASS = P * PACK
WORDS = K_PASS // 2
PASSES = 4
ROWS = 4096
H = 512
H_TILES = H // P
TILE_WORDS = PASSES * P
EPS = 0.0001

TILES = ROWS // P
GROUP_TILES = 4
GROUPS = TILES // GROUP_TILES
GROUP_BUFS = 4
STORE_TILES = 2

FLOPS = 2 * ROWS * PASSES * K_PASS * H


def as_words(tile_2d, row_tiles):
    return tile_2d[:].bitcast(F32).rearrange("p (t w) -> p t w", t=row_tiles)


def turn_into_bank(nc, turn_banks, identity, two_sources):
    turned = turn_banks.tile([P, 2, 2, P], F32)
    for i in range(2):
        for u in range(2):
            nc.tensor.transpose(
                out=turned[:, i, u, :],
                in_=two_sources[i][:, u * P : (u + 1) * P],
                identity=identity[:],
            )
    return turned


def empty_bank(turned, grouped_words, copy_out):
    copy_out(out=grouped_words, in_=turned[:].rearrange("p g u r -> p g r u"))


def tile_sparsegatedrnncell_pb_t_kernel(
    tc, x, hx, sy, internal, W_ih, W_hh, W_sh, mu, out
):
    nc = tc.nc

    by_group = "(g p t) k -> g p t k"
    x_groups = x.rearrange(by_group, p=P, t=GROUP_TILES)
    hx_groups = hx.rearrange(by_group, p=P, t=GROUP_TILES)
    sy_groups = sy.rearrange(by_group, p=P, t=GROUP_TILES)
    internal_groups = internal.rearrange(by_group, p=P, t=GROUP_TILES)
    out_groups = out.rearrange(by_group, p=P, t=GROUP_TILES)

    with ExitStack() as stack:
        stack.enter_context(tc.manual_schedule())
        consts = stack.enter_context(tc.tile_pool(name="consts", bufs=1))
        loads = stack.enter_context(tc.tile_pool(name="loads", bufs=GROUP_BUFS))
        regroup = stack.enter_context(tc.tile_pool(name="regroup", bufs=5))
        packed = stack.enter_context(tc.tile_pool(name="packed", bufs=4))
        results = stack.enter_context(tc.tile_pool(name="results", bufs=8))
        drives = stack.enter_context(tc.tile_pool(name="drives", bufs=GROUP_TILES))
        small = stack.enter_context(tc.tile_pool(name="small", bufs=6))
        turn_banks = stack.enter_context(tc.psum_pool(name="turn_banks", bufs=4))
        sum_banks = stack.enter_context(tc.psum_pool(name="sum_banks", bufs=4))

        groups = {}
        tiles = {i: {} for i in range(TILES)}

        def load_group(g, widths):
            x_sb = loads.tile([P, GROUP_TILES * K_PASS], BF16)
            hx_sb = loads.tile([P, GROUP_TILES * K_PASS], BF16)
            sy_sb = loads.tile([P, GROUP_TILES * 2 * K_PASS], BF16)
            internal_sb = loads.tile([P, GROUP_TILES, H], BF16)
            groups[g] = {
                "x": as_words(x_sb, GROUP_TILES),
                "hx": as_words(hx_sb, GROUP_TILES),
                "sy": as_words(sy_sb, GROUP_TILES),
                "internal": internal_sb,
            }
            first = 0
            for width in widths:
                t = slice(first, first + width)
                first += width
                for sb, dram in ((x_sb, x_groups), (hx_sb, hx_groups), (sy_sb, sy_groups)):
                    nc.sync.dma_start(
                        out=sb[:].rearrange("p (t k) -> p t k", t=GROUP_TILES)[:, t, :],
                        in_=dram[g][:, t, :],
                    )
            nc.sync.dma_start(out=internal_sb[:], in_=internal_groups[g])

        mu_row = consts.tile([P, H], BF16)
        nc.vector.memset(mu_row[:], 0.0)
        nc.scalar.dma_start(out=mu_row[0:1, :], in_=mu.rearrange("(o h) -> o h", o=1))
        ones = consts.tile([P, P], BF16)
        nc.vector.memset(ones[:], 1.0)

        w_ih_sb = consts.tile([P, H_TILES * K_PASS], BF16)
        w_hh_sb = consts.tile([P, H_TILES * K_PASS], BF16)
        w_sh_sb = consts.tile([P, H_TILES * 2 * K_PASS], BF16)
        for w_sb, w_dram, parts in ((w_ih_sb, W_ih, 1), (w_hh_sb, W_hh, 1), (w_sh_sb, W_sh, 2)):
            wide = H_TILES // parts
            for j in range(0, H_TILES, wide):
                nc.sync.dma_start(
                    out=w_sb[:].rearrange("p (j k) -> p j k", j=H_TILES)[:, j : j + wide, :],
                    in_=w_dram.rearrange("(p j) k -> p j k", j=H_TILES)[:, j : j + wide, :],
                )
        load_group(0, (1, 1, 2))
        for g in range(1, GROUP_BUFS - 1):
            load_group(g, (2, 2))
        load_group(GROUP_BUFS - 1, (GROUP_TILES,))

        identity = consts.tile([P, P], F32)
        make_identity(nc, identity[:])

        table_seed = consts.tile([P, 1], F32)
        nc.vector.memset(table_seed[:], 1.0)
        nc.scalar.sqrt(out=table_seed[:], in_=table_seed[:])

        w_grouped = consts.tile([P, PASSES * H * PACK], BF16, align_bytes=64)
        w_codes = consts.tile([P, PASSES * H], U32, align_bytes=64)
        w_scales = consts.tile([P, PASSES * H], U8, align_bytes=64)
        w_grouped_words = w_grouped[:].bitcast(F32).rearrange(
            "p (g r j u) -> p g r j u", g=PASSES, r=P, j=H_TILES, u=2
        )
        w_ih_words = as_words(w_ih_sb, H_TILES)
        w_hh_words = as_words(w_hh_sb, H_TILES)
        w_sh_words = as_words(w_sh_sb, H_TILES)
        w_words = (
            w_ih_words,
            w_hh_words,
            w_sh_words[:, :, 0:WORDS],
            w_sh_words[:, :, WORDS : 2 * WORDS],
        )
        filler = consts.tile([P, H], BF16)
        nc.vector.memset(filler[:], 0.0)
        filler_bank = sum_banks.tile([P, H], F32, tag="sums")

        def keep_tensor_clock_up(matmuls):
            for i in range(matmuls):
                nc.tensor.matmul(
                    out=filler_bank[:], lhsT=filler[:, 0:P], rhs=filler[:], start=True, stop=True
                )

        keep_tensor_clock_up(5)
        for g, j in ((0, 0), (0, 2), (1, 0), (1, 2), (2, 0), (3, 0), (2, 2), (3, 2)):
            turned = turn_into_bank(
                nc, turn_banks, identity, [w_words[g][:, j, :], w_words[g][:, j + 1, :]]
            )
            keep_tensor_clock_up(1)
            copy_out = nc.vector.tensor_copy if (g, j) in ((0, 2), (1, 2), (3, 0)) else nc.scalar.copy
            copy_out(
                out=w_grouped_words[:, g, :, j : j + 2, :],
                in_=turned[:].rearrange("p j u r -> p r j u"),
            )
            if j == 2:
                one_pass = slice(g * H, (g + 1) * H)
                nc.vector.quantize_mx(
                    out=w_codes[:, one_pass].bitcast(FP8X4),
                    scales=w_scales[:, one_pass],
                    in_=w_grouped[:, g * H * PACK : (g + 1) * H * PACK],
                )

        mu_all = consts.tile([P, H], F32)

        def spread_mu():
            mu_bank = sum_banks.tile([P, H], F32, tag="sums")
            nc.tensor.matmul(out=mu_bank[:], lhsT=ones[:], rhs=mu_row[:], start=True, stop=True)
            return mu_bank

        def new_grouped(i):
            grouped = regroup.tile([P, TILE_WORDS * PACK], BF16, align_bytes=64)
            tiles[i]["grouped"] = grouped

        def turn(i):
            group, t = groups[i // GROUP_TILES], i % GROUP_TILES
            four_passes = [
                group["x"][:, t, :],
                group["hx"][:, t, :],
                group["sy"][:, t, 0:WORDS],
                group["sy"][:, t, WORDS : 2 * WORDS],
            ]
            tiles[i]["turned"] = [
                turn_into_bank(nc, turn_banks, identity, four_passes[2 * pair : 2 * pair + 2])
                for pair in range(PASSES // 2)
            ]

        def regroup_pair(i, pair):
            grouped_words = tiles[i]["grouped"][:].bitcast(F32).rearrange(
                "p (g r u) -> p g r u", g=PASSES, r=P, u=2
            )
            empty_bank(
                tiles[i]["turned"][pair],
                grouped_words[:, 2 * pair : 2 * pair + 2, :, :],
                nc.scalar.copy,
            )

        def quantise(i):
            codes = packed.tile([P, TILE_WORDS], U32, align_bytes=64)
            scales = packed.tile([P, TILE_WORDS], U8, align_bytes=64)
            nc.vector.quantize_mx(
                out=codes[:].bitcast(FP8X4), scales=scales[:], in_=tiles[i]["grouped"][:]
            )
            tiles[i]["codes"], tiles[i]["scales"] = codes, scales

        def multiply(i):
            codes, scales = tiles[i]["codes"], tiles[i]["scales"]
            sums = sum_banks.tile([P, H], F32, tag="sums")
            for g in range(PASSES):
                rows = slice(g * P, (g + 1) * P)
                cols = slice(g * H, (g + 1) * H)
                nc.tensor.matmul_mx(
                    out=sums[:],
                    lhsT=codes[:, rows].bitcast(FP8X4),
                    lhsT_scale=scales[:, rows],
                    rhs=w_codes[:, cols].bitcast(FP8X4),
                    rhs_scale=w_scales[:, cols],
                    start=(g == 0),
                    stop=(g == PASSES - 1),
                )
            tiles[i]["sums"] = sums

        def add_mu_to_internal(i, add, mu_source):
            drive = drives.tile([P, H], F32)
            add(
                out=drive[:],
                in0=groups[i // GROUP_TILES]["internal"][:, i % GROUP_TILES, :],
                in1=mu_source[:],
                op=ALU.add,
            )
            tiles[i]["drive"] = drive

        def statistics(i):
            stats = small.tile([P, 6], F32)
            nc.vector.bn_stats(out=stats[:], in_=tiles[i]["sums"][:])
            tiles[i]["stats"] = stats

        def mean_and_variance(i):
            mean_var = small.tile([P, 2], F32)
            nc.vector.bn_aggr(out=mean_var[:], in_=tiles[i]["stats"][:])
            tiles[i]["mean_var"] = mean_var

        def standard_deviation(i):
            std = small.tile([P, 1], F32)
            nc.scalar.sqrt(out=std[:], in_=tiles[i]["mean_var"][:, 1:2])
            tiles[i]["std"] = std

        def add_eps(i):
            minus_std = small.tile([P, 1], F32)
            nc.scalar.activation(
                out=minus_std[:], in_=tiles[i]["std"][:], func=ACT.Copy, scale=-1.0, bias=-EPS
            )
            tiles[i]["minus_std"] = minus_std

        def invert(i):
            minus_inv = small.tile([P, 1], F32)
            nc.vector.reciprocal(out=minus_inv[:], in_=tiles[i]["minus_std"][:])
            tiles[i]["minus_inv"] = minus_inv

        def scale_and_add(i):
            if i % STORE_TILES == 0:
                minus_hy = results.tile([P, STORE_TILES, H], F32)
            else:
                minus_hy = tiles[i - 1]["minus_hy"]
            nc.vector.scalar_tensor_tensor(
                out=minus_hy[:, i % STORE_TILES, :],
                in0=tiles[i]["sums"][:],
                scalar=tiles[i]["minus_inv"][:],
                in1=tiles[i]["drive"][:],
                op0=ALU.mult,
                op1=ALU.subtract,
            )
            tiles[i]["minus_hy"] = minus_hy

        def shift_by_mean(i):
            shift = small.tile([P, 1], F32)
            nc.scalar.activation(
                out=shift[:], in_=tiles[i]["mean_var"][:, 0:1], func=ACT.Copy,
                scale=tiles[i]["minus_inv"][:],
            )
            tiles[i]["shift"] = shift

        def relu(i):
            hy = tiles[i]["minus_hy"][:, i % STORE_TILES, :]
            nc.scalar.activation(
                out=hy, in_=hy, func=ACT.Relu, bias=tiles[i]["shift"][:], scale=-1.0
            )

        def store(i, width):
            last, last_in_group = i % STORE_TILES + 1, i % GROUP_TILES + 1
            nc.sync.dma_start(
                out=out_groups[i // GROUP_TILES][:, last_in_group - width : last_in_group, :],
                in_=tiles[i]["minus_hy"][:, last - width : last, :],
            )

        def exists(i):
            return 0 <= i < TILES

        turn(0)
        new_grouped(0)
        regroup_pair(0, 0)
        regroup_pair(0, 1)
        turn(1)
        new_grouped(1)
        regroup_pair(1, 0)
        regroup_pair(1, 1)
        mu_bank = spread_mu()
        keep_tensor_clock_up(1)
        quantise(0)
        multiply(0)
        keep_tensor_clock_up(0)
        quantise(1)
        for i in (2, 3):
            turn(i)
            new_grouped(i)
            regroup_pair(i, 0)
            regroup_pair(i, 1)
        multiply(1)
        statistics(0)
        mean_and_variance(0)
        add_mu_to_internal(0, nc.vector.tensor_tensor, mu_bank)
        quantise(2)
        for i in range(1, GROUP_TILES):
            add_mu_to_internal(i, nc.vector.tensor_tensor, mu_bank)
        standard_deviation(0)
        add_eps(0)
        nc.scalar.copy(out=mu_all[:], in_=mu_bank[:])
        turn(4)
        new_grouped(4)
        regroup_pair(4, 0)
        regroup_pair(4, 1)

        for k in range(TILES + 3):
            if exists(k + 5):
                turn(k + 5)

            if k == 1:
                invert(0)
                scale_and_add(0)
            if exists(k + 3):
                quantise(k + 3)
            if 1 <= k < TILES - 1:
                mean_and_variance(k)
            if k > 1 and exists(k - 1):
                invert(k - 1)

            if exists(k - 2):
                shift_by_mean(k - 2)
            if exists(k + 5):
                new_grouped(k + 5)
                regroup_pair(k + 5, 0)
            if k >= 1 and exists(k):
                standard_deviation(k)
            if k == TILES - 1:
                add_eps(k)
            if exists(k - 2):
                relu(k - 2)
                if k - 2 >= TILES - 4:
                    store(k - 2, 1)
                elif (k - 1) % STORE_TILES == 0:
                    store(k - 2, STORE_TILES)
            if 1 <= k < TILES - 1:
                add_eps(k)
            if exists(k + 5):
                regroup_pair(k + 5, 1)

            if exists(k + 1):
                statistics(k + 1)
            if k + 1 == TILES - 1:
                mean_and_variance(k + 1)
            if k > 1 and exists(k - 1):
                scale_and_add(k - 1)

            if exists(k + 3) and k + 3 >= GROUP_TILES:
                add_mu_to_internal(k + 3, nc.gpsimd.tensor_tensor, mu_all)

            if exists(k + 2):
                multiply(k + 2)

            g = GROUP_BUFS + k // GROUP_TILES
            if k % GROUP_TILES == 0 and g < GROUPS:
                load_group(g, (GROUP_TILES,))
